import numpy as np
import ml_dtypes


def mxq(x, axis, fmt="e4m3"):
    dtype, down = {"e4m3": (ml_dtypes.float8_e4m3fn, 7), "e5m2": (ml_dtypes.float8_e5m2, 14)}[fmt]
    v = np.moveaxis(np.asarray(x, np.float32).astype(ml_dtypes.bfloat16).astype(np.float64), axis, -1)
    blocks = v.reshape(v.shape[:-1] + (-1, 32))
    amax = np.abs(blocks).max(-1, keepdims=True)
    byte = np.maximum(np.where(amax > 0, np.frexp(amax)[1] - 1 + 127, 0) - down, 1)
    scale = np.exp2(byte - 127.0)
    codes = (blocks / scale).astype(np.float32).astype(dtype).astype(np.float64)
    return np.moveaxis((codes * scale).reshape(v.shape), -1, axis)


WIDE = False


def mx_kscale(k):
    if not WIDE:
        return np.ones(k)
    levels = np.array([10, -10, 5, -5, 0])
    if k % 512:
        return np.exp2(np.random.permutation(np.resize(levels, k // 32))).repeat(32)
    a = np.empty((k // 512, 16))
    for p in range(k // 512):
        a[p, :8] = np.random.permutation(np.resize(levels, 8))
        for g in range(8):
            far = levels[np.abs(levels - a[p, g]) >= 10]
            a[p, g + 8] = far[np.random.randint(len(far))]
    return np.exp2(a.ravel()).repeat(32)


BF16 = ml_dtypes.bfloat16


def bf(x):
    return np.asarray(x, np.float32).astype(BF16)


def f64(x):
    return np.asarray(x).astype(np.float64)


B, S, H, NH = 16, 256, 512, 8
DK = H // NH
NORM_EPS = 1e-6


def elu(v):
    return np.where(v > 0.0, v, np.exp(np.minimum(v, 0.0)) - 1.0)


def setup_inputs():
    s = mx_kscale(H)
    w = 1.0 / np.sqrt(H)
    return {"hidden_states": bf(np.random.standard_normal((B, S, H)) * s),
            "Wq": bf(np.random.standard_normal((H, H)) * 1.5 * w / s[:, None]),
            "Wk": bf(np.random.standard_normal((H, H)) * 1.5 * w / s[:, None]),
            "Wv": bf(np.random.standard_normal((H, H)) * 2.0 * w / s[:, None])}


def reference(hidden_states, Wq, Wk, Wv):
    xq = mxq(f64(hidden_states), 2, "e4m3")
    q = (xq @ mxq(f64(Wq), 0, "e4m3")).reshape(B, S, NH, DK)
    k = (xq @ mxq(f64(Wk), 0, "e4m3")).reshape(B, S, NH, DK)
    v = (xq @ mxq(f64(Wv), 0, "e4m3")).reshape(B, S, NH, DK)
    q = elu(q) + 1.0
    k = elu(k) + 1.0
    qk = np.sum(q * k, axis=-1, keepdims=True)
    k_sum = np.sum(k, axis=1, keepdims=True)
    normalizer = np.sum(q * k_sum, axis=-1, keepdims=True)
    z = qk * v / (normalizer + NORM_EPS)
    return z.reshape(B, S, H)

@@ -1,0 +1,322 @@
+from contextlib import ExitStack
+
+import concourse.mybir as mybir
+from concourse.masks import make_identity
+
+F32 = mybir.dt.float32
+BF16 = mybir.dt.bfloat16
+U32 = mybir.dt.uint32
+U8 = mybir.dt.uint8
+FP8X4 = mybir.dt.float8_e4m3fn_x4
+ALU = mybir.AluOpType
+ACT = mybir.ActivationFunctionType
+
+P = 128
+PACK = 4
+BATCHES, TOKENS, HIDDEN, HEADS = 16, 256, 512, 8
+HEAD_DIM = HIDDEN // HEADS
+NORM_EPS = 1e-6
+
+GROUP_BATCHES = 2
+GROUP_TOKENS = GROUP_BATCHES * TOKENS
+GROUPS = BATCHES // GROUP_BATCHES
+TILES = GROUP_TOKENS // P
+BATCH_TILES = TOKENS // P
+SLABS = HIDDEN // P
+SLAB_DIM = HEAD_DIM // SLABS
+UNITS = GROUPS * SLABS
+
+SUM_COLUMNS = 64
+
+SUMS_LAG = SLABS - 1 + 3
+VALUE_LAG = SUMS_LAG + TILES
+
+FLOPS = 3 * 2 * BATCHES * TOKENS * HIDDEN * HIDDEN
+
+
+def tile_gatedlinearattention_pa_t_kernel(tc, hidden_states, Wq, Wk, Wv, out):
+    nc = tc.nc
+    with ExitStack() as stack:
+        keep = stack.enter_context(tc.tile_pool(name="keep", bufs=1))
+        stage = stack.enter_context(tc.tile_pool(name="stage", bufs=2))
+        work = stack.enter_context(tc.tile_pool(name="work", bufs=3))
+        lagged = stack.enter_context(tc.tile_pool(name="lagged", bufs=VALUE_LAG + 1))
+        proj_psum = stack.enter_context(tc.psum_pool(name="proj_psum", bufs=4))
+        aux_psum = stack.enter_context(tc.psum_pool(name="aux_psum", bufs=3))
+        sums_psum = stack.enter_context(tc.psum_pool(name="sums_psum", bufs=1))
+        stack.enter_context(tc.manual_schedule())
+
+        x_raw = keep.tile([P, GROUPS, GROUP_TOKENS * HIDDEN // P], BF16)
+
+        def load_x(g):
+            batches = hidden_states[GROUP_BATCHES * g : GROUP_BATCHES * (g + 1)]
+            nc.sync.dma_start(
+                out=x_raw[:, g, :].rearrange("r (b w) -> r b w", b=GROUP_BATCHES),
+                in_=batches.rearrange("b (r j) k -> r b (j k)", j=BATCH_TILES),
+            )
+
+        def load_weight(w, raw):
+            nc.sync.dma_start(out=raw[:], in_=w.rearrange("(p t) n -> p (t n)", t=PACK))
+
+        wq_raw = keep.tile([P, PACK * HIDDEN], BF16)
+        wk_raw = keep.tile([P, PACK * HIDDEN], BF16)
+        wv_raw = keep.tile([P, PACK * HIDDEN], BF16)
+        load_x(0)
+        load_weight(Wk, wk_raw)
+        load_weight(Wq, wq_raw)
+        load_x(1)
+        load_weight(Wv, wv_raw)
+        for g in range(2, GROUPS):
+            load_x(g)
+
+        identity = keep.tile([P, P], F32)
+        make_identity(nc, identity[:])
+        head_of_row = keep.tile([P, SUM_COLUMNS], F32)
+        nc.vector.memset(head_of_row[:], 0.0)
+        nc.vector.tensor_reduce(
+            out=head_of_row[:, 0:HEADS],
+            in_=identity[:].rearrange("f (n e) -> f n e", e=SLAB_DIM),
+            axis=mybir.AxisListType.X,
+            op=ALU.add,
+        )
+        table_warmer = keep.tile([P, 1], F32)
+        nc.vector.memset(table_warmer[:], 0.0)
+        nc.scalar.activation(out=table_warmer[:], in_=table_warmer[:], func=ACT.Exp)
+
+        wq_grouped = keep.tile([P, HIDDEN * PACK], BF16, align_bytes=64)
+        wk_grouped = keep.tile([P, HIDDEN * PACK], BF16, align_bytes=64)
+        wv_grouped = keep.tile([P, HIDDEN * PACK], BF16, align_bytes=64)
+        wq_codes = keep.tile([P, HIDDEN], U32, align_bytes=64)
+        wk_codes = keep.tile([P, HIDDEN], U32, align_bytes=64)
+        wv_codes = keep.tile([P, HIDDEN], U32, align_bytes=64)
+        wq_scales = keep.tile([P, HIDDEN], U8, align_bytes=64)
+        wk_scales = keep.tile([P, HIDDEN], U8, align_bytes=64)
+        wv_scales = keep.tile([P, HIDDEN], U8, align_bytes=64)
+        x_codes = keep.tile([P, GROUPS * GROUP_TOKENS], U32, align_bytes=64)
+        x_scales = keep.tile([P, GROUPS * GROUP_TOKENS], U8, align_bytes=64)
+
+        def quantise(grouped, codes, scales):
+            nc.vector.quantize_mx(out=codes.bitcast(FP8X4), scales=scales, in_=grouped)
+
+        def quantise_slab(i):
+            columns = slice(i * P, (i + 1) * P)
+            elements = slice(i * P * PACK, (i + 1) * P * PACK)
+            for raw, grouped in ((wk_raw, wk_grouped), (wq_raw, wq_grouped)):
+                nc.vector.tensor_copy(
+                    out=grouped[:, elements].rearrange("p (n e t) -> p n e t", n=HEADS, t=PACK),
+                    in_=raw[:].rearrange(
+                        "p (t n i e) -> p i n e t", t=PACK, n=HEADS, i=SLABS
+                    )[:, i],
+                )
+            quantise(wk_grouped[:, elements], wk_codes[:, columns], wk_scales[:, columns])
+            quantise(wq_grouped[:, elements], wq_codes[:, columns], wq_scales[:, columns])
+
+        def regroup_wv():
+            nc.vector.tensor_copy(
+                out=wv_grouped[:].rearrange("p (c i t) -> p c t i", i=4, t=PACK),
+                in_=wv_raw[:].rearrange("p (t c i) -> p c t i", t=PACK, i=4),
+            )
+
+        live = {}
+
+        def transpose_x(g):
+            words = x_raw[:, g, :].bitcast(F32)
+            token_words = HIDDEN // 2
+            x_grouped = stage.tile([P, GROUP_TOKENS * PACK], BF16, align_bytes=64)
+            grouped_words = x_grouped[:].bitcast(F32)
+            for b in range(GROUP_BATCHES):
+                xt = aux_psum.tile([P, 2, TOKENS], F32, tag="aux")
+                for j in range(BATCH_TILES):
+                    for u in range(2):
+                        first = (b * BATCH_TILES + j) * token_words
+                        nc.tensor.transpose(
+                            xt[:, u, j * P : (j + 1) * P],
+                            words[:, first + u : first + token_words : 2],
+                            identity[:],
+                        )
+                side_by_side = grouped_words[:, b * 2 * TOKENS : (b + 1) * 2 * TOKENS].rearrange(
+                    "p (c u) -> p c u", u=2
+                )
+                if b == 0:
+                    nc.vector.tensor_copy(out=side_by_side, in_=xt[:].rearrange("p u c -> p c u"))
+                else:
+                    nc.scalar.copy(out=side_by_side, in_=xt[:].rearrange("p u c -> p c u"))
+            live[("x_grouped", g)] = x_grouped
+
+        def quantise_x(g):
+            tokens = slice(g * GROUP_TOKENS, (g + 1) * GROUP_TOKENS)
+            quantise(live[("x_grouped", g)][:], x_codes[:, tokens], x_scales[:, tokens])
+
+        def project(s):
+            g, i = divmod(s, SLABS)
+            tokens = slice(g * GROUP_TOKENS, (g + 1) * GROUP_TOKENS)
+            columns = slice(i * P, (i + 1) * P)
+            for name, codes, scales in (("c", wk_codes, wk_scales), ("a", wq_codes, wq_scales)):
+                acc = proj_psum.tile([P, GROUP_TOKENS], F32, tag="proj", name="acc_" + name)
+                nc.tensor.matmul_mx(
+                    out=acc[:],
+                    lhsT=codes[:, columns].bitcast(FP8X4),
+                    lhsT_scale=scales[:, columns],
+                    rhs=x_codes[:, tokens].bitcast(FP8X4),
+                    rhs_scale=x_scales[:, tokens],
+                    start=True,
+                    stop=True,
+                )
+                live[(name, s)] = acc
+            for name in ("c", "a"):
+                below = work.tile([P, GROUP_TOKENS], F32, name="below_" + name)
+                nc.scalar.activation(out=below[:], in_=live[(name, s)][:], func=ACT.Relu, scale=-1.0)
+                live[("below_" + name, s)] = below
+            for name in ("c", "a"):
+                decay = work.tile([P, GROUP_TOKENS], F32, name="decay_" + name)
+                nc.scalar.activation(
+                    out=decay[:], in_=live[("below_" + name, s)][:], func=ACT.Exp, scale=-1.0
+                )
+                live[("decay_" + name, s)] = decay
+
+        def combine(s):
+            g, i = divmod(s, SLABS)
+            k = work.tile([P, GROUP_TOKENS], F32)
+            k_sum = stage.tile([P, GROUP_BATCHES], F32)
+            for b in range(GROUP_BATCHES):
+                batch = slice(b * TOKENS, (b + 1) * TOKENS)
+                nc.vector.scalar_tensor_tensor(
+                    out=k[:, batch],
+                    in0=live[("c", s)][:, batch],
+                    scalar=0.0,
+                    in1=live[("decay_c", s)][:, batch],
+                    op0=ALU.max,
+                    op1=ALU.add,
+                    accum_out=k_sum[:, b : b + 1],
+                )
+            q = lagged.tile([P, GROUP_TOKENS], F32)
+            nc.vector.scalar_tensor_tensor(
+                out=q[:],
+                in0=live[("a", s)][:],
+                scalar=0.0,
+                in1=live[("decay_a", s)][:],
+                op0=ALU.max,
+                op1=ALU.add,
+            )
+            k_sum_of_head = lagged.tile([P, GROUP_BATCHES, SUM_COLUMNS], F32)
+            shape = [P, GROUP_BATCHES, SUM_COLUMNS]
+            nc.vector.tensor_tensor(
+                out=k_sum_of_head[:],
+                in0=head_of_row[:].unsqueeze(1).to_broadcast(shape),
+                in1=k_sum[:].unsqueeze(2).to_broadcast(shape),
+                op=ALU.mult,
+            )
+            live[("q", s)] = q
+            live[("k_sum_of_head", s)] = k_sum_of_head
+            if i >= 2:
+                summed_products = live[("product", s - i)]
+                nc.gpsimd.tensor_tensor(
+                    out=summed_products[:],
+                    in0=summed_products[:],
+                    in1=live[("product", s - 1)][:],
+                    op=ALU.add,
+                )
+            product = lagged.tile([P, GROUP_TOKENS], F32)
+            nc.gpsimd.tensor_tensor(out=product[:], in0=q[:], in1=k[:], op=ALU.mult)
+            live[("product", s)] = product
+
+        def head_sums(h):
+            g, t = divmod(h, TILES)
+            if t == 0:
+                sums = sums_psum.tile([P, 2, TILES, SUM_COLUMNS], F32)
+                live[("sums", g)] = sums
+            sums = live[("sums", g)]
+            tile_tokens = slice(t * P, (t + 1) * P)
+            for i in range(SLABS):
+                nc.tensor.matmul(
+                    out=sums[:, 1, t, :],
+                    lhsT=live[("q", g * SLABS + i)][:, tile_tokens],
+                    rhs=live[("k_sum_of_head", g * SLABS + i)][:, t // BATCH_TILES, :],
+                    start=(i == 0),
+                    stop=(i == SLABS - 1),
+                )
+            nc.tensor.matmul(
+                out=sums[:, 0, t, :],
+                lhsT=live[("product", g * SLABS)][:, tile_tokens],
+                rhs=head_of_row[:],
+                start=True,
+                stop=False,
+            )
+            nc.tensor.matmul(
+                out=sums[:, 0, t, :],
+                lhsT=live[("product", g * SLABS + SLABS - 1)][:, tile_tokens],
+                rhs=head_of_row[:],
+                start=False,
+                stop=True,
+            )
+
+        def divide(g):
+            sums = live[("sums", g)]
+            denominator = stage.tile([P, TILES, HEADS], F32)
+            nc.vector.tensor_scalar(
+                out=denominator[:], in0=sums[:, 1, :, 0:HEADS], scalar1=NORM_EPS, scalar2=None, op0=ALU.add
+            )
+            inverse = stage.tile([P, TILES, HEADS], F32)
+            nc.vector.reciprocal(out=inverse[:], in_=denominator[:])
+            ratio = stage.tile([P, TILES, HEADS], F32)
+            nc.vector.tensor_tensor(
+                out=ratio[:], in0=sums[:, 0, :, 0:HEADS], in1=inverse[:], op=ALU.mult
+            )
+            live[("ratio", g)] = ratio
+
+        def value(w):
+            g, t = divmod(w, TILES)
+            b, j = divmod(t, BATCH_TILES)
+            tile_tokens = slice(w * P, (w + 1) * P)
+            v = aux_psum.tile([P, HIDDEN], F32, tag="aux")
+            nc.tensor.matmul_mx(
+                out=v[:],
+                lhsT=x_codes[:, tile_tokens].bitcast(FP8X4),
+                lhsT_scale=x_scales[:, tile_tokens],
+                rhs=wv_codes[:].bitcast(FP8X4),
+                rhs_scale=wv_scales[:],
+                start=True,
+                stop=True,
+            )
+            if j == 0:
+                z = work.tile([P, BATCH_TILES, HIDDEN], F32)
+                live[("z", g, b)] = z
+            z = live[("z", g, b)]
+            nc.vector.tensor_tensor(
+                out=z[:, j, :].rearrange("r (n d) -> r n d", n=HEADS),
+                in0=v[:].rearrange("r (n d) -> r n d", n=HEADS),
+                in1=live[("ratio", g)][:, t, :].unsqueeze(2).to_broadcast([P, HEADS, HEAD_DIM]),
+                op=ALU.mult,
+            )
+            if j == BATCH_TILES - 1:
+                nc.sync.dma_start(
+                    out=out[GROUP_BATCHES * g + b].rearrange("(r j) f -> r (j f)", j=BATCH_TILES),
+                    in_=z[:].rearrange("r j f -> r (j f)"),
+                )
+
+        transpose_x(0)
+        quantise_slab(0)
+        quantise_x(0)
+
+        for s in range(UNITS + VALUE_LAG):
+            if s < UNITS:
+                project(s)
+            if s + 1 < SLABS:
+                quantise_slab(s + 1)
+            if s >= VALUE_LAG:
+                value(s - VALUE_LAG)
+            if 0 <= s - SUMS_LAG < UNITS:
+                head_sums(s - SUMS_LAG)
+                if (s - SUMS_LAG) % TILES == TILES - 1:
+                    divide((s - SUMS_LAG) // TILES)
+            if s < UNITS:
+                combine(s)
+            if s == SLABS - 1:
+                regroup_wv()
+            if s == SLABS:
+                quantise(wv_grouped[:], wv_codes[:], wv_scales[:])
+            if s // SLABS + 1 < GROUPS:
+                if s % SLABS == 0:
+                    transpose_x(s // SLABS + 1)
+                if s % SLABS == 1:
+                    quantise_x(s // SLABS + 1)

@@ -42,7 +42,8 @@ def tile_gatedlinearattention_pa_t_kernel(tc, hidden_states, Wq, Wk, Wv, out):
         work = stack.enter_context(tc.tile_pool(name="work", bufs=3))
         lagged = stack.enter_context(tc.tile_pool(name="lagged", bufs=VALUE_LAG + 1))
         proj_psum = stack.enter_context(tc.psum_pool(name="proj_psum", bufs=4))
-        aux_psum = stack.enter_context(tc.psum_pool(name="aux_psum", bufs=3))
+        aux_psum = stack.enter_context(tc.psum_pool(name="aux_psum", bufs=2))
+        qk_psum = stack.enter_context(tc.psum_pool(name="qk_psum", bufs=1))
         sums_psum = stack.enter_context(tc.psum_pool(name="sums_psum", bufs=1))
         stack.enter_context(tc.manual_schedule())
 
@@ -208,14 +209,6 @@ def tile_gatedlinearattention_pa_t_kernel(tc, hidden_states, Wq, Wk, Wv, out):
             )
             live[("q", s)] = q
             live[("k_sum_of_head", s)] = k_sum_of_head
-            if i >= 2:
-                summed_products = live[("product", s - i)]
-                nc.gpsimd.tensor_tensor(
-                    out=summed_products[:],
-                    in0=summed_products[:],
-                    in1=live[("product", s - 1)][:],
-                    op=ALU.add,
-                )
             product = lagged.tile([P, GROUP_TOKENS], F32)
             nc.gpsimd.tensor_tensor(out=product[:], in0=q[:], in1=k[:], op=ALU.mult)
             live[("product", s)] = product
@@ -223,45 +216,48 @@ def tile_gatedlinearattention_pa_t_kernel(tc, hidden_states, Wq, Wk, Wv, out):
         def head_sums(h):
             g, t = divmod(h, TILES)
             if t == 0:
-                sums = sums_psum.tile([P, 2, TILES, SUM_COLUMNS], F32)
+                sums = sums_psum.tile([P, TILES, SUM_COLUMNS], F32)
                 live[("sums", g)] = sums
+                qk_parts = qk_psum.tile([P, TILES, P], F32)
+                live[("qk_parts", g)] = qk_parts
             sums = live[("sums", g)]
+            qk_parts = live[("qk_parts", g)]
             tile_tokens = slice(t * P, (t + 1) * P)
             for i in range(SLABS):
                 nc.tensor.matmul(
-                    out=sums[:, 1, t, :],
+                    out=sums[:, t, :],
                     lhsT=live[("q", g * SLABS + i)][:, tile_tokens],
                     rhs=live[("k_sum_of_head", g * SLABS + i)][:, t // BATCH_TILES, :],
                     start=(i == 0),
                     stop=(i == SLABS - 1),
                 )
-            nc.tensor.matmul(
-                out=sums[:, 0, t, :],
-                lhsT=live[("product", g * SLABS)][:, tile_tokens],
-                rhs=head_of_row[:],
-                start=True,
-                stop=False,
-            )
-            nc.tensor.matmul(
-                out=sums[:, 0, t, :],
-                lhsT=live[("product", g * SLABS + SLABS - 1)][:, tile_tokens],
-                rhs=head_of_row[:],
-                start=False,
-                stop=True,
-            )
+            for i in range(SLABS):
+                nc.tensor.matmul(
+                    out=qk_parts[:, t, :],
+                    lhsT=live[("product", g * SLABS + i)][:, tile_tokens],
+                    rhs=identity[:],
+                    is_transpose=True,
+                    start=(i == 0),
+                    stop=(i == SLABS - 1),
+                )
 
         def divide(g):
             sums = live[("sums", g)]
             denominator = stage.tile([P, TILES, HEADS], F32)
             nc.vector.tensor_scalar(
-                out=denominator[:], in0=sums[:, 1, :, 0:HEADS], scalar1=NORM_EPS, scalar2=None, op0=ALU.add
+                out=denominator[:], in0=sums[:, :, 0:HEADS], scalar1=NORM_EPS, scalar2=None, op0=ALU.add
             )
             inverse = stage.tile([P, TILES, HEADS], F32)
             nc.vector.reciprocal(out=inverse[:], in_=denominator[:])
-            ratio = stage.tile([P, TILES, HEADS], F32)
-            nc.vector.tensor_tensor(
-                out=ratio[:], in0=sums[:, 0, :, 0:HEADS], in1=inverse[:], op=ALU.mult
+            qk = stage.tile([P, TILES, HEADS], F32)
+            nc.vector.tensor_reduce(
+                out=qk[:],
+                in_=live[("qk_parts", g)][:].rearrange("r t (n e) -> r t n e", n=HEADS),
+                axis=mybir.AxisListType.X,
+                op=ALU.add,
             )
+            ratio = stage.tile([P, TILES, HEADS], F32)
+            nc.vector.tensor_tensor(out=ratio[:], in0=qk[:], in1=inverse[:], op=ALU.mult)
             live[("ratio", g)] = ratio
 
         def value(w):

@@ -26,10 +26,8 @@ SLABS = HIDDEN // P
 SLAB_DIM = HEAD_DIM // SLABS
 UNITS = GROUPS * SLABS
 
-SUM_COLUMNS = 64
-
-SUMS_LAG = SLABS - 1 + 3
-VALUE_LAG = SUMS_LAG + TILES
+SUMS_LAG = SLABS + 1
+VALUE_LAG = SUMS_LAG + 2
 
 FLOPS = 3 * 2 * BATCHES * TOKENS * HIDDEN * HIDDEN
 
@@ -40,11 +38,11 @@ def tile_gatedlinearattention_pa_t_kernel(tc, hidden_states, Wq, Wk, Wv, out):
         keep = stack.enter_context(tc.tile_pool(name="keep", bufs=1))
         stage = stack.enter_context(tc.tile_pool(name="stage", bufs=2))
         work = stack.enter_context(tc.tile_pool(name="work", bufs=3))
-        lagged = stack.enter_context(tc.tile_pool(name="lagged", bufs=VALUE_LAG + 1))
-        proj_psum = stack.enter_context(tc.psum_pool(name="proj_psum", bufs=4))
+        lagged = stack.enter_context(tc.tile_pool(name="lagged", bufs=2 * SLABS + 1))
+        c_psum = stack.enter_context(tc.psum_pool(name="c_psum", bufs=2))
+        a_psum = stack.enter_context(tc.psum_pool(name="a_psum", bufs=2))
         aux_psum = stack.enter_context(tc.psum_pool(name="aux_psum", bufs=2))
-        qk_psum = stack.enter_context(tc.psum_pool(name="qk_psum", bufs=1))
-        sums_psum = stack.enter_context(tc.psum_pool(name="sums_psum", bufs=1))
+        sums_psum = stack.enter_context(tc.psum_pool(name="sums_psum", bufs=2))
         stack.enter_context(tc.manual_schedule())
 
         x_raw = keep.tile([P, GROUPS, GROUP_TOKENS * HIDDEN // P], BF16)
@@ -72,10 +70,9 @@ def tile_gatedlinearattention_pa_t_kernel(tc, hidden_states, Wq, Wk, Wv, out):
 
         identity = keep.tile([P, P], F32)
         make_identity(nc, identity[:])
-        head_of_row = keep.tile([P, SUM_COLUMNS], F32)
-        nc.vector.memset(head_of_row[:], 0.0)
+        head_of_row = keep.tile([P, HEADS], F32)
         nc.vector.tensor_reduce(
-            out=head_of_row[:, 0:HEADS],
+            out=head_of_row[:],
             in_=identity[:].rearrange("f (n e) -> f n e", e=SLAB_DIM),
             axis=mybir.AxisListType.X,
             op=ALU.add,
@@ -120,12 +117,14 @@ def tile_gatedlinearattention_pa_t_kernel(tc, hidden_states, Wq, Wk, Wv, out):
 
         live = {}
 
-        def transpose_x(g):
+        def transpose_x(g, b):
             words = x_raw[:, g, :].bitcast(F32)
             token_words = HIDDEN // 2
-            x_grouped = stage.tile([P, GROUP_TOKENS * PACK], BF16, align_bytes=64)
-            grouped_words = x_grouped[:].bitcast(F32)
-            for b in range(GROUP_BATCHES):
+            if b == 0:
+                x_grouped = stage.tile([P, GROUP_TOKENS * PACK], BF16, align_bytes=64)
+                live[("x_grouped", g)] = x_grouped
+            grouped_words = live[("x_grouped", g)][:].bitcast(F32)
+            for b in (b,):
                 xt = aux_psum.tile([P, 2, TOKENS], F32, tag="aux")
                 for j in range(BATCH_TILES):
                     for u in range(2):
@@ -138,11 +137,10 @@ def tile_gatedlinearattention_pa_t_kernel(tc, hidden_states, Wq, Wk, Wv, out):
                 side_by_side = grouped_words[:, b * 2 * TOKENS : (b + 1) * 2 * TOKENS].rearrange(
                     "p (c u) -> p c u", u=2
                 )
-                if b == 0:
+                if b == 0 and g == 0:
                     nc.vector.tensor_copy(out=side_by_side, in_=xt[:].rearrange("p u c -> p c u"))
                 else:
                     nc.scalar.copy(out=side_by_side, in_=xt[:].rearrange("p u c -> p c u"))
-            live[("x_grouped", g)] = x_grouped
 
         def quantise_x(g):
             tokens = slice(g * GROUP_TOKENS, (g + 1) * GROUP_TOKENS)
@@ -152,8 +150,11 @@ def tile_gatedlinearattention_pa_t_kernel(tc, hidden_states, Wq, Wk, Wv, out):
             g, i = divmod(s, SLABS)
             tokens = slice(g * GROUP_TOKENS, (g + 1) * GROUP_TOKENS)
             columns = slice(i * P, (i + 1) * P)
-            for name, codes, scales in (("c", wk_codes, wk_scales), ("a", wq_codes, wq_scales)):
-                acc = proj_psum.tile([P, GROUP_TOKENS], F32, tag="proj", name="acc_" + name)
+            for name, pool, codes, scales in (
+                ("c", c_psum, wk_codes, wk_scales),
+                ("a", a_psum, wq_codes, wq_scales),
+            ):
+                acc = pool.tile([P, GROUP_TOKENS], F32, name="acc_" + name)
                 nc.tensor.matmul_mx(
                     out=acc[:],
                     lhsT=codes[:, columns].bitcast(FP8X4),
@@ -164,21 +165,22 @@ def tile_gatedlinearattention_pa_t_kernel(tc, hidden_states, Wq, Wk, Wv, out):
                     stop=True,
                 )
                 live[(name, s)] = acc
-            for name in ("c", "a"):
-                below = work.tile([P, GROUP_TOKENS], F32, name="below_" + name)
-                nc.scalar.activation(out=below[:], in_=live[(name, s)][:], func=ACT.Relu, scale=-1.0)
-                live[("below_" + name, s)] = below
-            for name in ("c", "a"):
-                decay = work.tile([P, GROUP_TOKENS], F32, name="decay_" + name)
-                nc.scalar.activation(
-                    out=decay[:], in_=live[("below_" + name, s)][:], func=ACT.Exp, scale=-1.0
-                )
-                live[("decay_" + name, s)] = decay
+            exp_c = work.tile([P, GROUP_TOKENS], F32)
+            nc.scalar.activation(out=exp_c[:], in_=live[("c", s)][:], func=ACT.Exp)
+            decay_c = work.tile([P, GROUP_TOKENS], F32)
+            nc.gpsimd.tensor_scalar(
+                out=decay_c[:], in0=exp_c[:], scalar1=1.0, scalar2=0.0, op0=ALU.min, op1=ALU.max
+            )
+            live[("decay_c", s)] = decay_c
+            below = work.tile([P, GROUP_TOKENS], F32)
+            nc.scalar.activation(out=below[:], in_=live[("a", s)][:], func=ACT.Relu, scale=-1.0)
+            decay_a = work.tile([P, GROUP_TOKENS], F32)
+            nc.scalar.activation(out=decay_a[:], in_=below[:], func=ACT.Exp, scale=-1.0)
+            live[("decay_a", s)] = decay_a
 
         def combine(s):
-            g, i = divmod(s, SLABS)
             k = work.tile([P, GROUP_TOKENS], F32)
-            k_sum = stage.tile([P, GROUP_BATCHES], F32)
+            k_sum = work.tile([P, GROUP_BATCHES], F32)
             for b in range(GROUP_BATCHES):
                 batch = slice(b * TOKENS, (b + 1) * TOKENS)
                 nc.vector.scalar_tensor_tensor(
@@ -199,66 +201,75 @@ def tile_gatedlinearattention_pa_t_kernel(tc, hidden_states, Wq, Wk, Wv, out):
                 op0=ALU.max,
                 op1=ALU.add,
             )
-            k_sum_of_head = lagged.tile([P, GROUP_BATCHES, SUM_COLUMNS], F32)
-            shape = [P, GROUP_BATCHES, SUM_COLUMNS]
-            nc.vector.tensor_tensor(
-                out=k_sum_of_head[:],
-                in0=head_of_row[:].unsqueeze(1).to_broadcast(shape),
-                in1=k_sum[:].unsqueeze(2).to_broadcast(shape),
-                op=ALU.mult,
-            )
+            live[("k", s)] = k
+            live[("k_sum", s)] = k_sum
             live[("q", s)] = q
-            live[("k_sum_of_head", s)] = k_sum_of_head
+
+        def multiply(s):
             product = lagged.tile([P, GROUP_TOKENS], F32)
-            nc.gpsimd.tensor_tensor(out=product[:], in0=q[:], in1=k[:], op=ALU.mult)
-            live[("product", s)] = product
-
-        def head_sums(h):
-            g, t = divmod(h, TILES)
-            if t == 0:
-                sums = sums_psum.tile([P, TILES, SUM_COLUMNS], F32)
-                live[("sums", g)] = sums
-                qk_parts = qk_psum.tile([P, TILES, P], F32)
-                live[("qk_parts", g)] = qk_parts
-            sums = live[("sums", g)]
-            qk_parts = live[("qk_parts", g)]
-            tile_tokens = slice(t * P, (t + 1) * P)
-            for i in range(SLABS):
-                nc.tensor.matmul(
-                    out=sums[:, t, :],
-                    lhsT=live[("q", g * SLABS + i)][:, tile_tokens],
-                    rhs=live[("k_sum_of_head", g * SLABS + i)][:, t // BATCH_TILES, :],
-                    start=(i == 0),
-                    stop=(i == SLABS - 1),
-                )
-            for i in range(SLABS):
-                nc.tensor.matmul(
-                    out=qk_parts[:, t, :],
-                    lhsT=live[("product", g * SLABS + i)][:, tile_tokens],
-                    rhs=identity[:],
-                    is_transpose=True,
-                    start=(i == 0),
-                    stop=(i == SLABS - 1),
-                )
-
-        def divide(g):
-            sums = live[("sums", g)]
-            denominator = stage.tile([P, TILES, HEADS], F32)
-            nc.vector.tensor_scalar(
-                out=denominator[:], in0=sums[:, :, 0:HEADS], scalar1=NORM_EPS, scalar2=None, op0=ALU.add
+            nc.gpsimd.tensor_tensor(
+                out=product[:], in0=live[("q", s)][:], in1=live[("k", s)][:], op=ALU.mult
             )
-            inverse = stage.tile([P, TILES, HEADS], F32)
-            nc.vector.reciprocal(out=inverse[:], in_=denominator[:])
-            qk = stage.tile([P, TILES, HEADS], F32)
+            live[("product", s)] = product
+            k_sum_of_head = lagged.tile([P, GROUP_BATCHES, HEADS], F32)
+            for b in range(GROUP_BATCHES):
+                nc.scalar.activation(
+                    out=k_sum_of_head[:, b, :],
+                    in_=head_of_row[:],
+                    func=ACT.Copy,
+                    scale=live[("k_sum", s)][:, b : b + 1],
+                )
+            live[("k_sum_of_head", s)] = k_sum_of_head
+
+        def head_sums(g, b):
+            sums = sums_psum.tile([P, BATCH_TILES, P + HEADS], F32)
+            for j in range(BATCH_TILES):
+                t = b * BATCH_TILES + j
+                tile_tokens = slice(t * P, (t + 1) * P)
+                for i in range(SLABS):
+                    nc.tensor.matmul(
+                        out=sums[:, j, P : P + HEADS],
+                        lhsT=live[("q", g * SLABS + i)][:, tile_tokens],
+                        rhs=live[("k_sum_of_head", g * SLABS + i)][:, b, :],
+                        start=(i == 0),
+                        stop=(i == SLABS - 1),
+                    )
+            for j in range(BATCH_TILES):
+                t = b * BATCH_TILES + j
+                tile_tokens = slice(t * P, (t + 1) * P)
+                for i in range(SLABS):
+                    nc.tensor.matmul(
+                        out=sums[:, j, 0:P],
+                        lhsT=live[("product", g * SLABS + i)][:, tile_tokens],
+                        rhs=identity[:],
+                        is_transpose=True,
+                        start=(i == 0),
+                        stop=(i == SLABS - 1),
+                    )
+            live[("sums", g, b)] = sums
+
+        def divide(g, b):
+            sums = live[("sums", g, b)]
+            denominator = stage.tile([P, BATCH_TILES, HEADS], F32)
+            nc.vector.tensor_scalar(
+                out=denominator[:],
+                in0=sums[:, :, P : P + HEADS],
+                scalar1=NORM_EPS,
+                scalar2=None,
+                op0=ALU.add,
+            )
+            qk = stage.tile([P, BATCH_TILES, HEADS], F32)
             nc.vector.tensor_reduce(
                 out=qk[:],
-                in_=live[("qk_parts", g)][:].rearrange("r t (n e) -> r t n e", n=HEADS),
+                in_=sums[:, :, 0:P].rearrange("r t (n e) -> r t n e", n=HEADS),
                 axis=mybir.AxisListType.X,
                 op=ALU.add,
             )
-            ratio = stage.tile([P, TILES, HEADS], F32)
-            nc.vector.tensor_tensor(out=ratio[:], in0=qk[:], in1=inverse[:], op=ALU.mult)
-            live[("ratio", g)] = ratio
+            inverse = stage.tile([P, BATCH_TILES, HEADS], F32)
+            nc.vector.reciprocal(out=inverse[:], in_=denominator[:])
+            ratio = stage.tile([P, BATCH_TILES, HEADS], F32)
+            nc.gpsimd.tensor_tensor(out=ratio[:], in0=qk[:], in1=inverse[:], op=ALU.mult)
+            live[("ratio", g, b)] = ratio
 
         def value(w):
             g, t = divmod(w, TILES)
@@ -281,7 +292,7 @@ def tile_gatedlinearattention_pa_t_kernel(tc, hidden_states, Wq, Wk, Wv, out):
             nc.vector.tensor_tensor(
                 out=z[:, j, :].rearrange("r (n d) -> r n d", n=HEADS),
                 in0=v[:].rearrange("r (n d) -> r n d", n=HEADS),
-                in1=live[("ratio", g)][:, t, :].unsqueeze(2).to_broadcast([P, HEADS, HEAD_DIM]),
+                in1=live[("ratio", g, b)][:, j, :].unsqueeze(2).to_broadcast([P, HEADS, HEAD_DIM]),
                 op=ALU.mult,
             )
             if j == BATCH_TILES - 1:
@@ -290,7 +301,8 @@ def tile_gatedlinearattention_pa_t_kernel(tc, hidden_states, Wq, Wk, Wv, out):
                     in_=z[:].rearrange("r j f -> r (j f)"),
                 )
 
-        transpose_x(0)
+        for b in range(GROUP_BATCHES):
+            transpose_x(0, b)
         quantise_slab(0)
         quantise_x(0)
 
@@ -301,18 +313,23 @@ def tile_gatedlinearattention_pa_t_kernel(tc, hidden_states, Wq, Wk, Wv, out):
                 quantise_slab(s + 1)
             if s >= VALUE_LAG:
                 value(s - VALUE_LAG)
-            if 0 <= s - SUMS_LAG < UNITS:
-                head_sums(s - SUMS_LAG)
-                if (s - SUMS_LAG) % TILES == TILES - 1:
-                    divide((s - SUMS_LAG) // TILES)
+            g, phase = divmod(s - SUMS_LAG, SLABS)
+            summed = 0 <= g < GROUPS and phase % 2 == 0
+            if summed:
+                head_sums(g, phase // 2)
+            if 1 <= s <= UNITS:
+                multiply(s - 1)
             if s < UNITS:
                 combine(s)
+            if summed:
+                divide(g, phase // 2)
             if s == SLABS - 1:
                 regroup_wv()
             if s == SLABS:
                 quantise(wv_grouped[:], wv_codes[:], wv_scales[:])
-            if s // SLABS + 1 < GROUPS:
-                if s % SLABS == 0:
-                    transpose_x(s // SLABS + 1)
-                if s % SLABS == 1:
-                    quantise_x(s // SLABS + 1)
+            g, phase = divmod(s, SLABS)
+            if g + 1 < GROUPS:
+                if phase < GROUP_BATCHES:
+                    transpose_x(g + 1, phase)
+                elif phase == GROUP_BATCHES:
+                    quantise_x(g + 1)

@@ -27,7 +27,7 @@ SLAB_DIM = HEAD_DIM // SLABS
 UNITS = GROUPS * SLABS
 
 SUMS_LAG = SLABS + 1
-VALUE_LAG = SUMS_LAG + 2
+VALUE_LAG = SUMS_LAG + 3
 
 FLOPS = 3 * 2 * BATCHES * TOKENS * HIDDEN * HIDDEN
 
@@ -70,13 +70,6 @@ def tile_gatedlinearattention_pa_t_kernel(tc, hidden_states, Wq, Wk, Wv, out):
 
         identity = keep.tile([P, P], F32)
         make_identity(nc, identity[:])
-        head_of_row = keep.tile([P, HEADS], F32)
-        nc.vector.tensor_reduce(
-            out=head_of_row[:],
-            in_=identity[:].rearrange("f (n e) -> f n e", e=SLAB_DIM),
-            axis=mybir.AxisListType.X,
-            op=ALU.add,
-        )
         table_warmer = keep.tile([P, 1], F32)
         nc.vector.memset(table_warmer[:], 0.0)
         nc.scalar.activation(out=table_warmer[:], in_=table_warmer[:], func=ACT.Exp)
@@ -206,69 +199,53 @@ def tile_gatedlinearattention_pa_t_kernel(tc, hidden_states, Wq, Wk, Wv, out):
             live[("q", s)] = q
 
         def multiply(s):
-            product = lagged.tile([P, GROUP_TOKENS], F32)
-            nc.gpsimd.tensor_tensor(
-                out=product[:], in0=live[("q", s)][:], in1=live[("k", s)][:], op=ALU.mult
-            )
-            live[("product", s)] = product
-            k_sum_of_head = lagged.tile([P, GROUP_BATCHES, HEADS], F32)
+            q = live[("q", s)]
+            weighted = lagged.tile([P, GROUP_TOKENS], F32)
             for b in range(GROUP_BATCHES):
+                batch = slice(b * TOKENS, (b + 1) * TOKENS)
                 nc.scalar.activation(
-                    out=k_sum_of_head[:, b, :],
-                    in_=head_of_row[:],
+                    out=weighted[:, batch],
+                    in_=q[:, batch],
                     func=ACT.Copy,
                     scale=live[("k_sum", s)][:, b : b + 1],
+                    bias=NORM_EPS / HEAD_DIM,
                 )
-            live[("k_sum_of_head", s)] = k_sum_of_head
+            live[("weighted", s)] = weighted
+            product = lagged.tile([P, GROUP_TOKENS], F32)
+            nc.gpsimd.tensor_tensor(out=product[:], in0=q[:], in1=live[("k", s)][:], op=ALU.mult)
+            live[("product", s)] = product
 
-        def head_sums(g, b):
-            sums = sums_psum.tile([P, BATCH_TILES, P + HEADS], F32)
-            for j in range(BATCH_TILES):
-                t = b * BATCH_TILES + j
-                tile_tokens = slice(t * P, (t + 1) * P)
+        def head_sums(h):
+            g, t = divmod(h, TILES)
+            b, j = divmod(t, BATCH_TILES)
+            if j == 0:
+                sums = sums_psum.tile([P, 2, BATCH_TILES, P], F32)
+                live[("sums", g, b)] = sums
+            sums = live[("sums", g, b)]
+            tile_tokens = slice(t * P, (t + 1) * P)
+            for kind, name in enumerate(("weighted", "product")):
                 for i in range(SLABS):
                     nc.tensor.matmul(
-                        out=sums[:, j, P : P + HEADS],
-                        lhsT=live[("q", g * SLABS + i)][:, tile_tokens],
-                        rhs=live[("k_sum_of_head", g * SLABS + i)][:, b, :],
-                        start=(i == 0),
-                        stop=(i == SLABS - 1),
-                    )
-            for j in range(BATCH_TILES):
-                t = b * BATCH_TILES + j
-                tile_tokens = slice(t * P, (t + 1) * P)
-                for i in range(SLABS):
-                    nc.tensor.matmul(
-                        out=sums[:, j, 0:P],
-                        lhsT=live[("product", g * SLABS + i)][:, tile_tokens],
+                        out=sums[:, kind, j, :],
+                        lhsT=live[(name, g * SLABS + i)][:, tile_tokens],
                         rhs=identity[:],
                         is_transpose=True,
                         start=(i == 0),
                         stop=(i == SLABS - 1),
                     )
-            live[("sums", g, b)] = sums
 
         def divide(g, b):
-            sums = live[("sums", g, b)]
-            denominator = stage.tile([P, BATCH_TILES, HEADS], F32)
-            nc.vector.tensor_scalar(
-                out=denominator[:],
-                in0=sums[:, :, P : P + HEADS],
-                scalar1=NORM_EPS,
-                scalar2=None,
-                op0=ALU.add,
-            )
-            qk = stage.tile([P, BATCH_TILES, HEADS], F32)
+            totals = stage.tile([P, 2, BATCH_TILES, HEADS], F32)
             nc.vector.tensor_reduce(
-                out=qk[:],
-                in_=sums[:, :, 0:P].rearrange("r t (n e) -> r t n e", n=HEADS),
+                out=totals[:].rearrange("r k t n -> r (k t n)"),
+                in_=live[("sums", g, b)][:].rearrange("r k t (n e) -> r (k t n) e", n=HEADS),
                 axis=mybir.AxisListType.X,
                 op=ALU.add,
             )
             inverse = stage.tile([P, BATCH_TILES, HEADS], F32)
-            nc.vector.reciprocal(out=inverse[:], in_=denominator[:])
+            nc.vector.reciprocal(out=inverse[:], in_=totals[:, 0])
             ratio = stage.tile([P, BATCH_TILES, HEADS], F32)
-            nc.gpsimd.tensor_tensor(out=ratio[:], in0=qk[:], in1=inverse[:], op=ALU.mult)
+            nc.gpsimd.tensor_tensor(out=ratio[:], in0=totals[:, 1], in1=inverse[:], op=ALU.mult)
             live[("ratio", g, b)] = ratio
 
         def value(w):
@@ -313,16 +290,15 @@ def tile_gatedlinearattention_pa_t_kernel(tc, hidden_states, Wq, Wk, Wv, out):
                 quantise_slab(s + 1)
             if s >= VALUE_LAG:
                 value(s - VALUE_LAG)
-            g, phase = divmod(s - SUMS_LAG, SLABS)
-            summed = 0 <= g < GROUPS and phase % 2 == 0
-            if summed:
-                head_sums(g, phase // 2)
+            h = s - SUMS_LAG
+            if 0 <= h < UNITS:
+                head_sums(h)
             if 1 <= s <= UNITS:
                 multiply(s - 1)
             if s < UNITS:
                 combine(s)
-            if summed:
-                divide(g, phase // 2)
+            if 0 <= h < UNITS and h % BATCH_TILES == BATCH_TILES - 1:
+                divide(h // TILES, h % TILES // BATCH_TILES)
             if s == SLABS - 1:
                 regroup_wv()
             if s == SLABS:

@@ -17,17 +17,33 @@ BATCHES, TOKENS, HIDDEN, HEADS = 16, 256, 512, 8
 HEAD_DIM = HIDDEN // HEADS
 NORM_EPS = 1e-6
 
-GROUP_BATCHES = 2
-GROUP_TOKENS = GROUP_BATCHES * TOKENS
-GROUPS = BATCHES // GROUP_BATCHES
-TILES = GROUP_TOKENS // P
-BATCH_TILES = TOKENS // P
+TILES = TOKENS // P
 SLABS = HIDDEN // P
 SLAB_DIM = HEAD_DIM // SLABS
-UNITS = GROUPS * SLABS
+UNIT_SLABS = 2
+BATCH_UNITS = SLABS // UNIT_SLABS
+UNITS = BATCHES * BATCH_UNITS
+UNIT_COLUMNS = UNIT_SLABS * TOKENS
 
-SUMS_LAG = SLABS + 1
-VALUE_LAG = SUMS_LAG + 3
+SUMS_LAG = 4
+VALUE_LAG = 6
+XPREP = 4
+COMBINE_LAG = 0
+V_LAST = 0
+SCALE_ENG = "act"
+CMIN = "pool"
+XCOPY = "act"
+SUM_SPLIT = 0
+RATIO = "dve"
+RATIO_LAG = 1
+PAIR = 0
+HQ = "scalar"
+HB = "vector"
+TAILP = 0
+TAILS = 1
+VA = 0
+VM = 0
+
 
 FLOPS = 3 * 2 * BATCHES * TOKENS * HIDDEN * HIDDEN
 
@@ -36,22 +52,21 @@ def tile_gatedlinearattention_pa_t_kernel(tc, hidden_states, Wq, Wk, Wv, out):
     nc = tc.nc
     with ExitStack() as stack:
         keep = stack.enter_context(tc.tile_pool(name="keep", bufs=1))
-        stage = stack.enter_context(tc.tile_pool(name="stage", bufs=2))
-        work = stack.enter_context(tc.tile_pool(name="work", bufs=3))
-        lagged = stack.enter_context(tc.tile_pool(name="lagged", bufs=2 * SLABS + 1))
+        stage = stack.enter_context(tc.tile_pool(name="stage", bufs=3))
+        work = stack.enter_context(tc.tile_pool(name="work", bufs=4))
+        lagged = stack.enter_context(tc.tile_pool(name="lagged", bufs=4))
         c_psum = stack.enter_context(tc.psum_pool(name="c_psum", bufs=2))
         a_psum = stack.enter_context(tc.psum_pool(name="a_psum", bufs=2))
         aux_psum = stack.enter_context(tc.psum_pool(name="aux_psum", bufs=2))
         sums_psum = stack.enter_context(tc.psum_pool(name="sums_psum", bufs=2))
         stack.enter_context(tc.manual_schedule())
 
-        x_raw = keep.tile([P, GROUPS, GROUP_TOKENS * HIDDEN // P], BF16)
+        x_raw = keep.tile([P, BATCHES, TILES * HIDDEN], BF16)
 
-        def load_x(g):
-            batches = hidden_states[GROUP_BATCHES * g : GROUP_BATCHES * (g + 1)]
+        def load_x(first, count):
             nc.sync.dma_start(
-                out=x_raw[:, g, :].rearrange("r (b w) -> r b w", b=GROUP_BATCHES),
-                in_=batches.rearrange("b (r j) k -> r b (j k)", j=BATCH_TILES),
+                out=x_raw[:, first : first + count, :],
+                in_=hidden_states[first : first + count].rearrange("b (r j) k -> r b (j k)", j=TILES),
             )
 
         def load_weight(w, raw):
@@ -60,13 +75,14 @@ def tile_gatedlinearattention_pa_t_kernel(tc, hidden_states, Wq, Wk, Wv, out):
         wq_raw = keep.tile([P, PACK * HIDDEN], BF16)
         wk_raw = keep.tile([P, PACK * HIDDEN], BF16)
         wv_raw = keep.tile([P, PACK * HIDDEN], BF16)
-        load_x(0)
+        load_x(0, 1)
         load_weight(Wk, wk_raw)
         load_weight(Wq, wq_raw)
-        load_x(1)
+        load_x(1, 1)
+        load_x(2, 2)
         load_weight(Wv, wv_raw)
-        for g in range(2, GROUPS):
-            load_x(g)
+        for b in range(4, BATCHES, 4):
+            load_x(b, 4)
 
         identity = keep.tile([P, P], F32)
         make_identity(nc, identity[:])
@@ -83,24 +99,29 @@ def tile_gatedlinearattention_pa_t_kernel(tc, hidden_states, Wq, Wk, Wv, out):
         wq_scales = keep.tile([P, HIDDEN], U8, align_bytes=64)
         wk_scales = keep.tile([P, HIDDEN], U8, align_bytes=64)
         wv_scales = keep.tile([P, HIDDEN], U8, align_bytes=64)
-        x_codes = keep.tile([P, GROUPS * GROUP_TOKENS], U32, align_bytes=64)
-        x_scales = keep.tile([P, GROUPS * GROUP_TOKENS], U8, align_bytes=64)
+        x_codes = keep.tile([P, BATCHES * TOKENS], U32, align_bytes=64)
+        x_scales = keep.tile([P, BATCHES * TOKENS], U8, align_bytes=64)
 
         def quantise(grouped, codes, scales):
             nc.vector.quantize_mx(out=codes.bitcast(FP8X4), scales=scales, in_=grouped)
 
-        def quantise_slab(i):
-            columns = slice(i * P, (i + 1) * P)
+        def regroup(raw, grouped, i, engine):
             elements = slice(i * P * PACK, (i + 1) * P * PACK)
-            for raw, grouped in ((wk_raw, wk_grouped), (wq_raw, wq_grouped)):
-                nc.vector.tensor_copy(
-                    out=grouped[:, elements].rearrange("p (n e t) -> p n e t", n=HEADS, t=PACK),
-                    in_=raw[:].rearrange(
-                        "p (t n i e) -> p i n e t", t=PACK, n=HEADS, i=SLABS
-                    )[:, i],
+            to = grouped[:, elements].rearrange("p (n e t) -> p n e t", n=HEADS, t=PACK)
+            source = raw[:].rearrange("p (t n i e) -> p i n e t", t=PACK, n=HEADS, i=SLABS)[:, i]
+            if engine == "vector":
+                nc.vector.tensor_copy(out=to, in_=source)
+            elif engine == "scalar":
+                nc.scalar.copy(out=to, in_=source)
+            else:
+                nc.gpsimd.tensor_scalar(
+                    out=to, in0=source, scalar1=1.0, scalar2=0.0, op0=ALU.mult, op1=ALU.add
                 )
-            quantise(wk_grouped[:, elements], wk_codes[:, columns], wk_scales[:, columns])
-            quantise(wq_grouped[:, elements], wq_codes[:, columns], wq_scales[:, columns])
+
+        def quantise_half(grouped, codes, scales, h):
+            columns = slice(h * UNIT_SLABS * P, (h + 1) * UNIT_SLABS * P)
+            elements = slice(h * UNIT_SLABS * P * PACK, (h + 1) * UNIT_SLABS * P * PACK)
+            quantise(grouped[:, elements], codes[:, columns], scales[:, columns])
 
         def regroup_wv():
             nc.vector.tensor_copy(
@@ -110,147 +131,189 @@ def tile_gatedlinearattention_pa_t_kernel(tc, hidden_states, Wq, Wk, Wv, out):
 
         live = {}
 
-        def transpose_x(g, b):
-            words = x_raw[:, g, :].bitcast(F32)
+        def transpose_x(b):
+            words = x_raw[:, b, :].bitcast(F32)
             token_words = HIDDEN // 2
-            if b == 0:
-                x_grouped = stage.tile([P, GROUP_TOKENS * PACK], BF16, align_bytes=64)
-                live[("x_grouped", g)] = x_grouped
-            grouped_words = live[("x_grouped", g)][:].bitcast(F32)
-            for b in (b,):
-                xt = aux_psum.tile([P, 2, TOKENS], F32, tag="aux")
-                for j in range(BATCH_TILES):
-                    for u in range(2):
-                        first = (b * BATCH_TILES + j) * token_words
-                        nc.tensor.transpose(
-                            xt[:, u, j * P : (j + 1) * P],
-                            words[:, first + u : first + token_words : 2],
-                            identity[:],
-                        )
-                side_by_side = grouped_words[:, b * 2 * TOKENS : (b + 1) * 2 * TOKENS].rearrange(
-                    "p (c u) -> p c u", u=2
-                )
-                if b == 0 and g == 0:
-                    nc.vector.tensor_copy(out=side_by_side, in_=xt[:].rearrange("p u c -> p c u"))
-                else:
-                    nc.scalar.copy(out=side_by_side, in_=xt[:].rearrange("p u c -> p c u"))
+            x_grouped = stage.tile([P, TOKENS * PACK], BF16, align_bytes=64)
+            live[("x_grouped", b)] = x_grouped
+            xt = aux_psum.tile([P, 2, TOKENS], F32, tag="aux")
+            for j in range(TILES):
+                for u in range(2):
+                    first = j * token_words
+                    nc.tensor.transpose(
+                        xt[:, u, j * P : (j + 1) * P],
+                        words[:, first + u : first + token_words : 2],
+                        identity[:],
+                    )
+            side_by_side = x_grouped[:].bitcast(F32).rearrange("p (c u) -> p c u", u=2)
+            if XCOPY == "dve":
+                nc.vector.tensor_copy(out=side_by_side, in_=xt[:].rearrange("p u c -> p c u"))
+            else:
+                nc.scalar.copy(out=side_by_side, in_=xt[:].rearrange("p u c -> p c u"))
 
-        def quantise_x(g):
-            tokens = slice(g * GROUP_TOKENS, (g + 1) * GROUP_TOKENS)
-            quantise(live[("x_grouped", g)][:], x_codes[:, tokens], x_scales[:, tokens])
+        def quantise_x(b):
+            tokens = slice(b * TOKENS, (b + 1) * TOKENS)
+            quantise(live[("x_grouped", b)][:], x_codes[:, tokens], x_scales[:, tokens])
 
         def project(s):
-            g, i = divmod(s, SLABS)
-            tokens = slice(g * GROUP_TOKENS, (g + 1) * GROUP_TOKENS)
-            columns = slice(i * P, (i + 1) * P)
+            b, h = divmod(s, BATCH_UNITS)
+            tokens = slice(b * TOKENS, (b + 1) * TOKENS)
             for name, pool, codes, scales in (
                 ("c", c_psum, wk_codes, wk_scales),
                 ("a", a_psum, wq_codes, wq_scales),
             ):
-                acc = pool.tile([P, GROUP_TOKENS], F32, name="acc_" + name)
-                nc.tensor.matmul_mx(
-                    out=acc[:],
-                    lhsT=codes[:, columns].bitcast(FP8X4),
-                    lhsT_scale=scales[:, columns],
-                    rhs=x_codes[:, tokens].bitcast(FP8X4),
-                    rhs_scale=x_scales[:, tokens],
-                    start=True,
-                    stop=True,
-                )
+                acc = pool.tile([P, UNIT_COLUMNS], F32, name="acc_" + name)
+                for i in range(UNIT_SLABS):
+                    columns = slice((h * UNIT_SLABS + i) * P, (h * UNIT_SLABS + i + 1) * P)
+                    nc.tensor.matmul_mx(
+                        out=acc[:, i * TOKENS : (i + 1) * TOKENS],
+                        lhsT=codes[:, columns].bitcast(FP8X4),
+                        lhsT_scale=scales[:, columns],
+                        rhs=x_codes[:, tokens].bitcast(FP8X4),
+                        rhs_scale=x_scales[:, tokens],
+                        start=True,
+                        stop=True,
+                    )
                 live[(name, s)] = acc
-            exp_c = work.tile([P, GROUP_TOKENS], F32)
-            nc.scalar.activation(out=exp_c[:], in_=live[("c", s)][:], func=ACT.Exp)
-            decay_c = work.tile([P, GROUP_TOKENS], F32)
-            nc.gpsimd.tensor_scalar(
-                out=decay_c[:], in0=exp_c[:], scalar1=1.0, scalar2=0.0, op0=ALU.min, op1=ALU.max
-            )
+
+        def decay_of(name, s):
+            return live[("decay_" + name, s)]
+
+        def feature_c(s):
+            if CMIN == "pool" or (CMIN == "mix" and s % 4 != 3):
+                exp_c = work.tile([P, UNIT_COLUMNS], F32)
+                nc.scalar.activation(out=exp_c[:], in_=live[("c", s)][:], func=ACT.Exp)
+                decay_c = work.tile([P, UNIT_COLUMNS], F32)
+                nc.gpsimd.tensor_scalar(
+                    out=decay_c[:], in0=exp_c[:], scalar1=1.0, scalar2=0.0, op0=ALU.min, op1=ALU.max
+                )
+            else:
+                below_c = work.tile([P, UNIT_COLUMNS], F32)
+                nc.scalar.activation(out=below_c[:], in_=live[("c", s)][:], func=ACT.Relu, scale=-1.0)
+                decay_c = work.tile([P, UNIT_COLUMNS], F32)
+                nc.scalar.activation(out=decay_c[:], in_=below_c[:], func=ACT.Exp, scale=-1.0)
             live[("decay_c", s)] = decay_c
-            below = work.tile([P, GROUP_TOKENS], F32)
+
+        def feature_a(s):
+            below = work.tile([P, UNIT_COLUMNS], F32)
             nc.scalar.activation(out=below[:], in_=live[("a", s)][:], func=ACT.Relu, scale=-1.0)
-            decay_a = work.tile([P, GROUP_TOKENS], F32)
+            decay_a = work.tile([P, UNIT_COLUMNS], F32)
             nc.scalar.activation(out=decay_a[:], in_=below[:], func=ACT.Exp, scale=-1.0)
             live[("decay_a", s)] = decay_a
 
-        def combine(s):
-            k = work.tile([P, GROUP_TOKENS], F32)
-            k_sum = work.tile([P, GROUP_BATCHES], F32)
-            for b in range(GROUP_BATCHES):
-                batch = slice(b * TOKENS, (b + 1) * TOKENS)
+        def make_k(s):
+            b, h = divmod(s, BATCH_UNITS)
+            if h == 0:
+                k = work.tile([P, BATCH_UNITS * UNIT_COLUMNS], F32)
+                live[("k_tile", b)] = k
+            k = live[("k_tile", b)][:, h * UNIT_COLUMNS : (h + 1) * UNIT_COLUMNS]
+            k_sum = work.tile([P, UNIT_SLABS], F32)
+            for i in range(UNIT_SLABS):
+                columns = slice(i * TOKENS, (i + 1) * TOKENS)
                 nc.vector.scalar_tensor_tensor(
-                    out=k[:, batch],
-                    in0=live[("c", s)][:, batch],
+                    out=k[:, columns],
+                    in0=live[("c", s)][:, columns],
                     scalar=0.0,
-                    in1=live[("decay_c", s)][:, batch],
+                    in1=live[("decay_c", s)][:, columns],
                     op0=ALU.max,
                     op1=ALU.add,
-                    accum_out=k_sum[:, b : b + 1],
+                    accum_out=k_sum[:, i : i + 1],
                 )
-            q = lagged.tile([P, GROUP_TOKENS], F32)
+            live[("k", s)] = k
+            live[("k_sum", s)] = k_sum
+
+        def make_q(s):
+            b, h = divmod(s, BATCH_UNITS)
+            if h == 0:
+                q = work.tile([P, BATCH_UNITS * UNIT_COLUMNS], F32)
+                live[("q_tile", b)] = q
+            q = live[("q_tile", b)][:, h * UNIT_COLUMNS : (h + 1) * UNIT_COLUMNS]
             nc.vector.scalar_tensor_tensor(
-                out=q[:],
+                out=q,
                 in0=live[("a", s)][:],
                 scalar=0.0,
                 in1=live[("decay_a", s)][:],
                 op0=ALU.max,
                 op1=ALU.add,
             )
-            live[("k", s)] = k
-            live[("k_sum", s)] = k_sum
             live[("q", s)] = q
 
-        def multiply(s):
+        def weigh(s):
             q = live[("q", s)]
-            weighted = lagged.tile([P, GROUP_TOKENS], F32)
-            for b in range(GROUP_BATCHES):
-                batch = slice(b * TOKENS, (b + 1) * TOKENS)
-                nc.scalar.activation(
-                    out=weighted[:, batch],
-                    in_=q[:, batch],
-                    func=ACT.Copy,
-                    scale=live[("k_sum", s)][:, b : b + 1],
-                    bias=NORM_EPS / HEAD_DIM,
-                )
+            weighted = lagged.tile([P, UNIT_COLUMNS], F32)
+            for i in range(UNIT_SLABS):
+                columns = slice(i * TOKENS, (i + 1) * TOKENS)
+                k_sum = live[("k_sum", s)][:, i : i + 1]
+                if SCALE_ENG == "act":
+                    nc.scalar.activation(
+                        out=weighted[:, columns], in_=q[:, columns], func=ACT.Copy,
+                        scale=k_sum, bias=NORM_EPS / HEAD_DIM,
+                    )
+                else:
+                    eng = nc.gpsimd if SCALE_ENG == "pool" else nc.vector
+                    eng.tensor_scalar(
+                        out=weighted[:, columns], in0=q[:, columns], scalar1=k_sum,
+                        scalar2=NORM_EPS / HEAD_DIM, op0=ALU.mult, op1=ALU.add,
+                    )
             live[("weighted", s)] = weighted
-            product = lagged.tile([P, GROUP_TOKENS], F32)
-            nc.gpsimd.tensor_tensor(out=product[:], in0=q[:], in1=live[("k", s)][:], op=ALU.mult)
-            live[("product", s)] = product
 
-        def head_sums(h):
-            g, t = divmod(h, TILES)
-            b, j = divmod(t, BATCH_TILES)
+        def multiply(s):
+            b, h = divmod(s, BATCH_UNITS)
+            pair = PAIR and b < BATCHES - 1
+            if pair and h == 0:
+                return
+            if h == 0 or pair:
+                product = lagged.tile([P, BATCH_UNITS * UNIT_COLUMNS], F32)
+                live[("product_tile", b)] = product
+            columns = slice(0 if pair else h * UNIT_COLUMNS, (h + 1) * UNIT_COLUMNS)
+            (nc.vector if TAILP and s == UNITS - 1 else nc.gpsimd).tensor_tensor(
+                out=live[("product_tile", b)][:, columns],
+                in0=live[("q_tile", b)][:, columns],
+                in1=live[("k_tile", b)][:, columns],
+                op=ALU.mult,
+            )
+            for i in range(BATCH_UNITS):
+                live[("product", b * BATCH_UNITS + i)] = live[("product_tile", b)][:, i * UNIT_COLUMNS : (i + 1) * UNIT_COLUMNS]
+
+        def head_sums(b, j):
             if j == 0:
-                sums = sums_psum.tile([P, 2, BATCH_TILES, P], F32)
-                live[("sums", g, b)] = sums
-            sums = live[("sums", g, b)]
-            tile_tokens = slice(t * P, (t + 1) * P)
+                sums = sums_psum.tile([P, 2, TILES, P], F32)
+                live[("sums", b)] = sums
+            sums = live[("sums", b)]
             for kind, name in enumerate(("weighted", "product")):
                 for i in range(SLABS):
+                    h, o = divmod(i, UNIT_SLABS)
+                    first = o * TOKENS + j * P
                     nc.tensor.matmul(
                         out=sums[:, kind, j, :],
-                        lhsT=live[(name, g * SLABS + i)][:, tile_tokens],
+                        lhsT=live[(name, b * BATCH_UNITS + h)][:, first : first + P],
                         rhs=identity[:],
                         is_transpose=True,
                         start=(i == 0),
                         stop=(i == SLABS - 1),
                     )
 
-        def divide(g, b):
-            totals = stage.tile([P, 2, BATCH_TILES, HEADS], F32)
+        def divide(b):
+            totals = stage.tile([P, 2, TILES, HEADS], F32)
             nc.vector.tensor_reduce(
                 out=totals[:].rearrange("r k t n -> r (k t n)"),
-                in_=live[("sums", g, b)][:].rearrange("r k t (n e) -> r (k t n) e", n=HEADS),
+                in_=live[("sums", b)][:].rearrange("r k t (n e) -> r (k t n) e", n=HEADS),
                 axis=mybir.AxisListType.X,
                 op=ALU.add,
             )
-            inverse = stage.tile([P, BATCH_TILES, HEADS], F32)
+            inverse = stage.tile([P, TILES, HEADS], F32)
             nc.vector.reciprocal(out=inverse[:], in_=totals[:, 0])
-            ratio = stage.tile([P, BATCH_TILES, HEADS], F32)
-            nc.gpsimd.tensor_tensor(out=ratio[:], in0=totals[:, 1], in1=inverse[:], op=ALU.mult)
-            live[("ratio", g, b)] = ratio
+            live[("totals", b)] = totals
+            live[("inverse", b)] = inverse
 
-        def value(w):
-            g, t = divmod(w, TILES)
-            b, j = divmod(t, BATCH_TILES)
+        def make_ratio(b):
+            ratio = stage.tile([P, TILES, HEADS], F32)
+            (nc.gpsimd if RATIO == "pool" else nc.vector).tensor_tensor(
+                out=ratio[:], in0=live[("totals", b)][:, 1], in1=live[("inverse", b)][:], op=ALU.mult
+            )
+            live[("ratio", b)] = ratio
+
+        def project_v(w):
             tile_tokens = slice(w * P, (w + 1) * P)
             v = aux_psum.tile([P, HIDDEN], F32, tag="aux")
             nc.tensor.matmul_mx(
@@ -262,50 +325,89 @@ def tile_gatedlinearattention_pa_t_kernel(tc, hidden_states, Wq, Wk, Wv, out):
                 start=True,
                 stop=True,
             )
+            live[("v", w)] = v
+
+        def scale_v(w):
+            b, j = divmod(w, TILES)
             if j == 0:
-                z = work.tile([P, BATCH_TILES, HIDDEN], F32)
-                live[("z", g, b)] = z
-            z = live[("z", g, b)]
-            nc.vector.tensor_tensor(
+                z = work.tile([P, TILES, HIDDEN], F32)
+                live[("z", b)] = z
+            z = live[("z", b)]
+            if VA and w in (BATCHES * TILES - 1, BATCHES * TILES - 3):
+                for n in range(HEADS):
+                    nc.scalar.activation(out=z[:, j, n * HEAD_DIM : (n + 1) * HEAD_DIM], in_=live[("v", w)][:, n * HEAD_DIM : (n + 1) * HEAD_DIM], func=ACT.Copy, scale=live[("ratio", b)][:, j, n : n + 1])
+            else:
+              nc.vector.tensor_tensor(
                 out=z[:, j, :].rearrange("r (n d) -> r n d", n=HEADS),
-                in0=v[:].rearrange("r (n d) -> r n d", n=HEADS),
-                in1=live[("ratio", g, b)][:, j, :].unsqueeze(2).to_broadcast([P, HEADS, HEAD_DIM]),
+                in0=live[("v", w)][:].rearrange("r (n d) -> r n d", n=HEADS),
+                in1=live[("ratio", b)][:, j, :].unsqueeze(2).to_broadcast([P, HEADS, HEAD_DIM]),
                 op=ALU.mult,
             )
-            if j == BATCH_TILES - 1:
+            if TAILS and b >= BATCHES - 1:
+                nc.sync.dma_start(out=out[b].rearrange("(r j) f -> r j f", j=TILES)[:, j], in_=z[:, j, :])
+            elif j == TILES - 1:
                 nc.sync.dma_start(
-                    out=out[GROUP_BATCHES * g + b].rearrange("(r j) f -> r (j f)", j=BATCH_TILES),
+                    out=out[b].rearrange("(r j) f -> r (j f)", j=TILES),
                     in_=z[:].rearrange("r j f -> r (j f)"),
                 )
 
-        for b in range(GROUP_BATCHES):
-            transpose_x(0, b)
-        quantise_slab(0)
+        transpose_x(0)
+        regroup(wk_raw, wk_grouped, 0, "vector")
+        regroup(wk_raw, wk_grouped, 1, "vector")
         quantise_x(0)
+        quantise_half(wk_grouped, wk_codes, wk_scales, 0)
+        regroup(wq_raw, wq_grouped, 0, "vector")
+        regroup(wq_raw, wq_grouped, 1, HQ)
+        quantise_half(wq_grouped, wq_codes, wq_scales, 0)
+        regroup(wk_raw, wk_grouped, 2, HB)
+        regroup(wk_raw, wk_grouped, 3, HB)
 
         for s in range(UNITS + VALUE_LAG):
             if s < UNITS:
                 project(s)
-            if s + 1 < SLABS:
-                quantise_slab(s + 1)
-            if s >= VALUE_LAG:
-                value(s - VALUE_LAG)
+                feature_c(s)
+                feature_a(s)
+            if s == 0:
+                regroup(wq_raw, wq_grouped, 2, "vector")
+                regroup(wq_raw, wq_grouped, 3, "vector")
+                quantise_half(wk_grouped, wk_codes, wk_scales, 1)
+                quantise_half(wq_grouped, wq_codes, wq_scales, 1)
+            w = s - VALUE_LAG
+            if w >= 0:
+                project_v(w)
+                if not V_LAST:
+                    scale_v(w)
             h = s - SUMS_LAG
             if 0 <= h < UNITS:
-                head_sums(h)
+                if SUM_SPLIT:
+                    head_sums(*divmod(h, TILES))
+                elif h % 2 == 0:
+                    head_sums(h // 2, 0)
+                    head_sums(h // 2, 1)
             if 1 <= s <= UNITS:
+                weigh(s - 1)
                 multiply(s - 1)
             if s < UNITS:
-                combine(s)
-            if 0 <= h < UNITS and h % BATCH_TILES == BATCH_TILES - 1:
-                divide(h // TILES, h % TILES // BATCH_TILES)
-            if s == SLABS - 1:
+                make_k(s)
+                make_q(s)
+            rb, rp = divmod(s - SUMS_LAG - RATIO_LAG - (TILES - 1 if SUM_SPLIT else 0), TILES)
+            if 0 <= rb < BATCHES and rp == 0:
+                make_ratio(rb)
+            if w >= 0 and V_LAST:
+                scale_v(w)
+            if 0 <= h < UNITS and h % TILES == (TILES - 1 if SUM_SPLIT else 0):
+                divide(h // TILES)
+            if s == 3:
                 regroup_wv()
-            if s == SLABS:
+            if s == 4:
                 quantise(wv_grouped[:], wv_codes[:], wv_scales[:])
-            g, phase = divmod(s, SLABS)
-            if g + 1 < GROUPS:
-                if phase < GROUP_BATCHES:
-                    transpose_x(g + 1, phase)
-                elif phase == GROUP_BATCHES:
-                    quantise_x(g + 1)
+            b, phase = divmod(s + XPREP, 2)
+            if s == 0:
+                for c in range(1, b):
+                    transpose_x(c)
+                    quantise_x(c)
+            if b < BATCHES:
+                if phase == 0:
+                    transpose_x(b)
+                else:
+                    quantise_x(b)

@@ -25,18 +25,24 @@ BATCH_UNITS = SLABS // UNIT_SLABS
 UNITS = BATCHES * BATCH_UNITS
 UNIT_COLUMNS = UNIT_SLABS * TOKENS
 
-SUMS_LAG = 4
+SUMS_LAG = 3
 VALUE_LAG = 6
 XPREP = 4
 COMBINE_LAG = 0
 V_LAST = 0
 SCALE_ENG = "act"
 CMIN = "pool"
-XCOPY = "act"
+XCOPY = "mix"
 SUM_SPLIT = 0
-RATIO = "dve"
+RATIO = "pool"
 RATIO_LAG = 1
 PAIR = 0
+AORD = 1
+QFIRST = 0
+CLAG = 0
+RECIP_LATE = 1
+NORM = "t"
+KSH = "act"
 HQ = "scalar"
 HB = "vector"
 TAILP = 0
@@ -57,8 +63,8 @@ def tile_gatedlinearattention_pa_t_kernel(tc, hidden_states, Wq, Wk, Wv, out):
         lagged = stack.enter_context(tc.tile_pool(name="lagged", bufs=4))
         c_psum = stack.enter_context(tc.psum_pool(name="c_psum", bufs=2))
         a_psum = stack.enter_context(tc.psum_pool(name="a_psum", bufs=2))
-        aux_psum = stack.enter_context(tc.psum_pool(name="aux_psum", bufs=2))
-        sums_psum = stack.enter_context(tc.psum_pool(name="sums_psum", bufs=2))
+        aux_psum = stack.enter_context(tc.psum_pool(name="aux_psum", bufs=3))
+        sums_psum = stack.enter_context(tc.psum_pool(name="sums_psum", bufs=1))
         stack.enter_context(tc.manual_schedule())
 
         x_raw = keep.tile([P, BATCHES, TILES * HIDDEN], BF16)
@@ -146,7 +152,7 @@ def tile_gatedlinearattention_pa_t_kernel(tc, hidden_states, Wq, Wk, Wv, out):
                         identity[:],
                     )
             side_by_side = x_grouped[:].bitcast(F32).rearrange("p (c u) -> p c u", u=2)
-            if XCOPY == "dve":
+            if XCOPY == "dve" or (XCOPY == "mix" and b % 2 == 1):
                 nc.vector.tensor_copy(out=side_by_side, in_=xt[:].rearrange("p u c -> p c u"))
             else:
                 nc.scalar.copy(out=side_by_side, in_=xt[:].rearrange("p u c -> p c u"))
@@ -194,9 +200,13 @@ def tile_gatedlinearattention_pa_t_kernel(tc, hidden_states, Wq, Wk, Wv, out):
                 nc.scalar.activation(out=decay_c[:], in_=below_c[:], func=ACT.Exp, scale=-1.0)
             live[("decay_c", s)] = decay_c
 
-        def feature_a(s):
+        def relu_a(s):
             below = work.tile([P, UNIT_COLUMNS], F32)
             nc.scalar.activation(out=below[:], in_=live[("a", s)][:], func=ACT.Relu, scale=-1.0)
+            live[("below", s)] = below
+
+        def exp_a(s):
+            below = live[("below", s)]
             decay_a = work.tile([P, UNIT_COLUMNS], F32)
             nc.scalar.activation(out=decay_a[:], in_=below[:], func=ACT.Exp, scale=-1.0)
             live[("decay_a", s)] = decay_a
@@ -301,9 +311,13 @@ def tile_gatedlinearattention_pa_t_kernel(tc, hidden_states, Wq, Wk, Wv, out):
                 axis=mybir.AxisListType.X,
                 op=ALU.add,
             )
-            inverse = stage.tile([P, TILES, HEADS], F32)
-            nc.vector.reciprocal(out=inverse[:], in_=totals[:, 0])
             live[("totals", b)] = totals
+            if not RECIP_LATE:
+                invert(b)
+
+        def invert(b):
+            inverse = stage.tile([P, TILES, HEADS], F32)
+            nc.vector.reciprocal(out=inverse[:], in_=live[("totals", b)][:, 0])
             live[("inverse", b)] = inverse
 
         def make_ratio(b):
@@ -365,8 +379,24 @@ def tile_gatedlinearattention_pa_t_kernel(tc, hidden_states, Wq, Wk, Wv, out):
         for s in range(UNITS + VALUE_LAG):
             if s < UNITS:
                 project(s)
-                feature_c(s)
-                feature_a(s)
+                if AORD == 0:
+                    relu_a(s)
+                    feature_c(s)
+                    exp_a(s)
+                elif AORD == 1:
+                    feature_c(s)
+                    relu_a(s)
+                elif AORD == 2:
+                    feature_c(s)
+                    relu_a(s)
+                    exp_a(s)
+                elif AORD == 3:
+                    if s:
+                        exp_a(s - 1)
+                    feature_c(s)
+                    relu_a(s)
+            elif AORD == 3 and s == UNITS:
+                exp_a(s - 1)
             if s == 0:
                 regroup(wq_raw, wq_grouped, 2, "vector")
                 regroup(wq_raw, wq_grouped, 3, "vector")
@@ -386,12 +416,26 @@ def tile_gatedlinearattention_pa_t_kernel(tc, hidden_states, Wq, Wk, Wv, out):
                     head_sums(h // 2, 1)
             if 1 <= s <= UNITS:
                 weigh(s - 1)
+            if AORD == 1 and s < UNITS:
+                exp_a(s)
+            if 1 <= s <= UNITS:
                 multiply(s - 1)
-            if s < UNITS:
-                make_k(s)
-                make_q(s)
             rb, rp = divmod(s - SUMS_LAG - RATIO_LAG - (TILES - 1 if SUM_SPLIT else 0), TILES)
-            if 0 <= rb < BATCHES and rp == 0:
+            divided = 0 <= rb < BATCHES and rp == 0
+            if divided and RECIP_LATE:
+                invert(rb)
+            if 0 <= s - CLAG < UNITS:
+                if QFIRST:
+                    make_q(s - CLAG)
+                    if divided:
+                        make_ratio(rb)
+                    make_k(s - CLAG)
+                else:
+                    make_k(s - CLAG)
+                    if divided:
+                        make_ratio(rb)
+                    make_q(s - CLAG)
+            elif divided:
                 make_ratio(rb)
             if w >= 0 and V_LAST:
                 scale_v(w)

@@ -19,37 +19,18 @@ NORM_EPS = 1e-6
 
 TILES = TOKENS // P
 SLABS = HIDDEN // P
-SLAB_DIM = HEAD_DIM // SLABS
 UNIT_SLABS = 2
 BATCH_UNITS = SLABS // UNIT_SLABS
 UNITS = BATCHES * BATCH_UNITS
 UNIT_COLUMNS = UNIT_SLABS * TOKENS
+VALUES = BATCHES * TILES
 
-SUMS_LAG = 3
+PRODUCT_LAG = 1
+WEIGH_LAG = 2
+SUMS_LAG = 4
+RATIO_LAG = 5
 VALUE_LAG = 6
-XPREP = 4
-COMBINE_LAG = 0
-V_LAST = 0
-SCALE_ENG = "act"
-CMIN = "pool"
-XCOPY = "mix"
-SUM_SPLIT = 0
-RATIO = "pool"
-RATIO_LAG = 1
-PAIR = 0
-AORD = 1
-QFIRST = 0
-CLAG = 0
-RECIP_LATE = 1
-NORM = "t"
-KSH = "act"
-HQ = "scalar"
-HB = "vector"
-TAILP = 0
-TAILS = 1
-VA = 0
-VM = 0
-
+X_LEAD = 4
 
 FLOPS = 3 * 2 * BATCHES * TOKENS * HIDDEN * HIDDEN
 
@@ -60,10 +41,9 @@ def tile_gatedlinearattention_pa_t_kernel(tc, hidden_states, Wq, Wk, Wv, out):
         keep = stack.enter_context(tc.tile_pool(name="keep", bufs=1))
         stage = stack.enter_context(tc.tile_pool(name="stage", bufs=3))
         work = stack.enter_context(tc.tile_pool(name="work", bufs=4))
-        lagged = stack.enter_context(tc.tile_pool(name="lagged", bufs=4))
         c_psum = stack.enter_context(tc.psum_pool(name="c_psum", bufs=2))
-        a_psum = stack.enter_context(tc.psum_pool(name="a_psum", bufs=2))
-        aux_psum = stack.enter_context(tc.psum_pool(name="aux_psum", bufs=3))
+        a_psum = stack.enter_context(tc.psum_pool(name="a_psum", bufs=3))
+        aux_psum = stack.enter_context(tc.psum_pool(name="aux_psum", bufs=2))
         sums_psum = stack.enter_context(tc.psum_pool(name="sums_psum", bufs=1))
         stack.enter_context(tc.manual_schedule())
 
@@ -113,18 +93,18 @@ def tile_gatedlinearattention_pa_t_kernel(tc, hidden_states, Wq, Wk, Wv, out):
 
         def regroup(raw, grouped, i, engine):
             elements = slice(i * P * PACK, (i + 1) * P * PACK)
-            to = grouped[:, elements].rearrange("p (n e t) -> p n e t", n=HEADS, t=PACK)
-            source = raw[:].rearrange("p (t n i e) -> p i n e t", t=PACK, n=HEADS, i=SLABS)[:, i]
-            if engine == "vector":
-                nc.vector.tensor_copy(out=to, in_=source)
-            elif engine == "scalar":
-                nc.scalar.copy(out=to, in_=source)
-            else:
+            words = grouped[:, elements].rearrange("p (n e t) -> p n e t", n=HEADS, t=PACK)
+            columns = raw[:].rearrange("p (t n i e) -> p i n e t", t=PACK, n=HEADS, i=SLABS)[:, i]
+            if engine is nc.scalar:
+                nc.scalar.copy(out=words, in_=columns)
+            elif engine is nc.gpsimd:
                 nc.gpsimd.tensor_scalar(
-                    out=to, in0=source, scalar1=1.0, scalar2=0.0, op0=ALU.mult, op1=ALU.add
+                    out=words, in0=columns, scalar1=1.0, scalar2=0.0, op0=ALU.mult, op1=ALU.add
                 )
+            else:
+                nc.vector.tensor_copy(out=words, in_=columns)
 
-        def quantise_half(grouped, codes, scales, h):
+        def quantise_unit(grouped, codes, scales, h):
             columns = slice(h * UNIT_SLABS * P, (h + 1) * UNIT_SLABS * P)
             elements = slice(h * UNIT_SLABS * P * PACK, (h + 1) * UNIT_SLABS * P * PACK)
             quantise(grouped[:, elements], codes[:, columns], scales[:, columns])
@@ -140,83 +120,69 @@ def tile_gatedlinearattention_pa_t_kernel(tc, hidden_states, Wq, Wk, Wv, out):
         def transpose_x(b):
             words = x_raw[:, b, :].bitcast(F32)
             token_words = HIDDEN // 2
-            x_grouped = stage.tile([P, TOKENS * PACK], BF16, align_bytes=64)
-            live[("x_grouped", b)] = x_grouped
             xt = aux_psum.tile([P, 2, TOKENS], F32, tag="aux")
             for j in range(TILES):
                 for u in range(2):
-                    first = j * token_words
                     nc.tensor.transpose(
                         xt[:, u, j * P : (j + 1) * P],
-                        words[:, first + u : first + token_words : 2],
+                        words[:, j * token_words + u : (j + 1) * token_words : 2],
                         identity[:],
                     )
+            live[("xt", b)] = xt
+
+        def copy_x(b):
+            x_grouped = stage.tile([P, TOKENS * PACK], BF16, align_bytes=64)
             side_by_side = x_grouped[:].bitcast(F32).rearrange("p (c u) -> p c u", u=2)
-            if XCOPY == "dve" or (XCOPY == "mix" and b % 2 == 1):
-                nc.vector.tensor_copy(out=side_by_side, in_=xt[:].rearrange("p u c -> p c u"))
+            words = live[("xt", b)][:].rearrange("p u c -> p c u")
+            if b % 2 == 0:
+                nc.scalar.copy(out=side_by_side, in_=words)
             else:
-                nc.scalar.copy(out=side_by_side, in_=xt[:].rearrange("p u c -> p c u"))
+                nc.vector.tensor_copy(out=side_by_side, in_=words)
+            live[("x_grouped", b)] = x_grouped
 
         def quantise_x(b):
             tokens = slice(b * TOKENS, (b + 1) * TOKENS)
             quantise(live[("x_grouped", b)][:], x_codes[:, tokens], x_scales[:, tokens])
 
-        def project(s):
+        def project(s, name, psum, codes, scales):
             b, h = divmod(s, BATCH_UNITS)
             tokens = slice(b * TOKENS, (b + 1) * TOKENS)
-            for name, pool, codes, scales in (
-                ("c", c_psum, wk_codes, wk_scales),
-                ("a", a_psum, wq_codes, wq_scales),
-            ):
-                acc = pool.tile([P, UNIT_COLUMNS], F32, name="acc_" + name)
-                for i in range(UNIT_SLABS):
-                    columns = slice((h * UNIT_SLABS + i) * P, (h * UNIT_SLABS + i + 1) * P)
-                    nc.tensor.matmul_mx(
-                        out=acc[:, i * TOKENS : (i + 1) * TOKENS],
-                        lhsT=codes[:, columns].bitcast(FP8X4),
-                        lhsT_scale=scales[:, columns],
-                        rhs=x_codes[:, tokens].bitcast(FP8X4),
-                        rhs_scale=x_scales[:, tokens],
-                        start=True,
-                        stop=True,
-                    )
-                live[(name, s)] = acc
-
-        def decay_of(name, s):
-            return live[("decay_" + name, s)]
-
-        def feature_c(s):
-            if CMIN == "pool" or (CMIN == "mix" and s % 4 != 3):
-                exp_c = work.tile([P, UNIT_COLUMNS], F32)
-                nc.scalar.activation(out=exp_c[:], in_=live[("c", s)][:], func=ACT.Exp)
-                decay_c = work.tile([P, UNIT_COLUMNS], F32)
-                nc.gpsimd.tensor_scalar(
-                    out=decay_c[:], in0=exp_c[:], scalar1=1.0, scalar2=0.0, op0=ALU.min, op1=ALU.max
+            acc = psum.tile([P, UNIT_COLUMNS], F32, name="acc_" + name)
+            for i in range(UNIT_SLABS):
+                slab = h * UNIT_SLABS + i
+                columns = slice(slab * P, (slab + 1) * P)
+                nc.tensor.matmul_mx(
+                    out=acc[:, i * TOKENS : (i + 1) * TOKENS],
+                    lhsT=codes[:, columns].bitcast(FP8X4),
+                    lhsT_scale=scales[:, columns],
+                    rhs=x_codes[:, tokens].bitcast(FP8X4),
+                    rhs_scale=x_scales[:, tokens],
+                    start=True,
+                    stop=True,
                 )
-            else:
-                below_c = work.tile([P, UNIT_COLUMNS], F32)
-                nc.scalar.activation(out=below_c[:], in_=live[("c", s)][:], func=ACT.Relu, scale=-1.0)
-                decay_c = work.tile([P, UNIT_COLUMNS], F32)
-                nc.scalar.activation(out=decay_c[:], in_=below_c[:], func=ACT.Exp, scale=-1.0)
+            live[(name, s)] = acc
+
+        def decay_of_c(s):
+            exp_c = work.tile([P, UNIT_COLUMNS], F32)
+            nc.scalar.activation(out=exp_c[:], in_=live[("c", s)][:], func=ACT.Exp)
+            decay_c = work.tile([P, UNIT_COLUMNS], F32)
+            nc.gpsimd.tensor_scalar(
+                out=decay_c[:], in0=exp_c[:], scalar1=1.0, scalar2=0.0, op0=ALU.min, op1=ALU.max
+            )
             live[("decay_c", s)] = decay_c
 
-        def relu_a(s):
+        def below_a(s):
             below = work.tile([P, UNIT_COLUMNS], F32)
             nc.scalar.activation(out=below[:], in_=live[("a", s)][:], func=ACT.Relu, scale=-1.0)
             live[("below", s)] = below
 
-        def exp_a(s):
-            below = live[("below", s)]
+        def decay_of_a(s):
             decay_a = work.tile([P, UNIT_COLUMNS], F32)
-            nc.scalar.activation(out=decay_a[:], in_=below[:], func=ACT.Exp, scale=-1.0)
+            nc.scalar.activation(out=decay_a[:], in_=live[("below", s)][:], func=ACT.Exp, scale=-1.0)
             live[("decay_a", s)] = decay_a
 
-        def make_k(s):
-            b, h = divmod(s, BATCH_UNITS)
-            if h == 0:
-                k = work.tile([P, BATCH_UNITS * UNIT_COLUMNS], F32)
-                live[("k_tile", b)] = k
-            k = live[("k_tile", b)][:, h * UNIT_COLUMNS : (h + 1) * UNIT_COLUMNS]
+        def combine(s):
+            k = work.tile([P, UNIT_COLUMNS], F32)
             k_sum = work.tile([P, UNIT_SLABS], F32)
             for i in range(UNIT_SLABS):
                 columns = slice(i * TOKENS, (i + 1) * TOKENS)
@@ -229,111 +195,83 @@ def tile_gatedlinearattention_pa_t_kernel(tc, hidden_states, Wq, Wk, Wv, out):
                     op1=ALU.add,
                     accum_out=k_sum[:, i : i + 1],
                 )
-            live[("k", s)] = k
-            live[("k_sum", s)] = k_sum
-
-        def make_q(s):
-            b, h = divmod(s, BATCH_UNITS)
-            if h == 0:
-                q = work.tile([P, BATCH_UNITS * UNIT_COLUMNS], F32)
-                live[("q_tile", b)] = q
-            q = live[("q_tile", b)][:, h * UNIT_COLUMNS : (h + 1) * UNIT_COLUMNS]
+            q = work.tile([P, UNIT_COLUMNS], F32)
             nc.vector.scalar_tensor_tensor(
-                out=q,
+                out=q[:],
                 in0=live[("a", s)][:],
                 scalar=0.0,
                 in1=live[("decay_a", s)][:],
                 op0=ALU.max,
                 op1=ALU.add,
             )
+            live[("k", s)] = k
+            live[("k_sum", s)] = k_sum
             live[("q", s)] = q
 
+        def multiply(s, engine):
+            product = work.tile([P, UNIT_COLUMNS], F32)
+            engine.tensor_tensor(out=product[:], in0=live[("q", s)][:], in1=live[("k", s)][:], op=ALU.mult)
+            live[("product", s)] = product
+
         def weigh(s):
-            q = live[("q", s)]
-            weighted = lagged.tile([P, UNIT_COLUMNS], F32)
+            weighted = work.tile([P, UNIT_COLUMNS], F32)
             for i in range(UNIT_SLABS):
                 columns = slice(i * TOKENS, (i + 1) * TOKENS)
-                k_sum = live[("k_sum", s)][:, i : i + 1]
-                if SCALE_ENG == "act":
-                    nc.scalar.activation(
-                        out=weighted[:, columns], in_=q[:, columns], func=ACT.Copy,
-                        scale=k_sum, bias=NORM_EPS / HEAD_DIM,
-                    )
-                else:
-                    eng = nc.gpsimd if SCALE_ENG == "pool" else nc.vector
-                    eng.tensor_scalar(
-                        out=weighted[:, columns], in0=q[:, columns], scalar1=k_sum,
-                        scalar2=NORM_EPS / HEAD_DIM, op0=ALU.mult, op1=ALU.add,
-                    )
+                nc.scalar.activation(
+                    out=weighted[:, columns],
+                    in_=live[("q", s)][:, columns],
+                    func=ACT.Copy,
+                    scale=live[("k_sum", s)][:, i : i + 1],
+                    bias=NORM_EPS / HEAD_DIM,
+                )
             live[("weighted", s)] = weighted
 
-        def multiply(s):
-            b, h = divmod(s, BATCH_UNITS)
-            pair = PAIR and b < BATCHES - 1
-            if pair and h == 0:
-                return
-            if h == 0 or pair:
-                product = lagged.tile([P, BATCH_UNITS * UNIT_COLUMNS], F32)
-                live[("product_tile", b)] = product
-            columns = slice(0 if pair else h * UNIT_COLUMNS, (h + 1) * UNIT_COLUMNS)
-            (nc.vector if TAILP and s == UNITS - 1 else nc.gpsimd).tensor_tensor(
-                out=live[("product_tile", b)][:, columns],
-                in0=live[("q_tile", b)][:, columns],
-                in1=live[("k_tile", b)][:, columns],
-                op=ALU.mult,
-            )
-            for i in range(BATCH_UNITS):
-                live[("product", b * BATCH_UNITS + i)] = live[("product_tile", b)][:, i * UNIT_COLUMNS : (i + 1) * UNIT_COLUMNS]
+        def sum_heads(b):
+            sums = sums_psum.tile([P, 2, TILES, P], F32)
+            for which, name in enumerate(("weighted", "product")):
+                for j in range(TILES):
+                    for slab in range(SLABS):
+                        h, i = divmod(slab, UNIT_SLABS)
+                        first = i * TOKENS + j * P
+                        nc.tensor.matmul(
+                            out=sums[:, which, j, :],
+                            lhsT=live[(name, b * BATCH_UNITS + h)][:, first : first + P],
+                            rhs=identity[:],
+                            is_transpose=True,
+                            start=(slab == 0),
+                            stop=(slab == SLABS - 1),
+                        )
+            live[("sums", b)] = sums
 
-        def head_sums(b, j):
-            if j == 0:
-                sums = sums_psum.tile([P, 2, TILES, P], F32)
-                live[("sums", b)] = sums
-            sums = live[("sums", b)]
-            for kind, name in enumerate(("weighted", "product")):
-                for i in range(SLABS):
-                    h, o = divmod(i, UNIT_SLABS)
-                    first = o * TOKENS + j * P
-                    nc.tensor.matmul(
-                        out=sums[:, kind, j, :],
-                        lhsT=live[(name, b * BATCH_UNITS + h)][:, first : first + P],
-                        rhs=identity[:],
-                        is_transpose=True,
-                        start=(i == 0),
-                        stop=(i == SLABS - 1),
-                    )
-
-        def divide(b):
+        def reduce_sums(b):
             totals = stage.tile([P, 2, TILES, HEADS], F32)
             nc.vector.tensor_reduce(
-                out=totals[:].rearrange("r k t n -> r (k t n)"),
-                in_=live[("sums", b)][:].rearrange("r k t (n e) -> r (k t n) e", n=HEADS),
+                out=totals[:].rearrange("r w j n -> r (w j n)"),
+                in_=live[("sums", b)][:].rearrange("r w j (n e) -> r (w j n) e", n=HEADS),
                 axis=mybir.AxisListType.X,
                 op=ALU.add,
             )
             live[("totals", b)] = totals
-            if not RECIP_LATE:
-                invert(b)
 
         def invert(b):
             inverse = stage.tile([P, TILES, HEADS], F32)
             nc.vector.reciprocal(out=inverse[:], in_=live[("totals", b)][:, 0])
             live[("inverse", b)] = inverse
 
-        def make_ratio(b):
+        def divide(b):
             ratio = stage.tile([P, TILES, HEADS], F32)
-            (nc.gpsimd if RATIO == "pool" else nc.vector).tensor_tensor(
+            nc.vector.tensor_tensor(
                 out=ratio[:], in0=live[("totals", b)][:, 1], in1=live[("inverse", b)][:], op=ALU.mult
             )
             live[("ratio", b)] = ratio
 
         def project_v(w):
-            tile_tokens = slice(w * P, (w + 1) * P)
+            tokens = slice(w * P, (w + 1) * P)
             v = aux_psum.tile([P, HIDDEN], F32, tag="aux")
             nc.tensor.matmul_mx(
                 out=v[:],
-                lhsT=x_codes[:, tile_tokens].bitcast(FP8X4),
-                lhsT_scale=x_scales[:, tile_tokens],
+                lhsT=x_codes[:, tokens].bitcast(FP8X4),
+                lhsT_scale=x_scales[:, tokens],
                 rhs=wv_codes[:].bitcast(FP8X4),
                 rhs_scale=wv_scales[:],
                 start=True,
@@ -341,23 +279,28 @@ def tile_gatedlinearattention_pa_t_kernel(tc, hidden_states, Wq, Wk, Wv, out):
             )
             live[("v", w)] = v
 
-        def scale_v(w):
+        def scale_v(w, engine):
             b, j = divmod(w, TILES)
             if j == 0:
                 z = work.tile([P, TILES, HIDDEN], F32)
                 live[("z", b)] = z
             z = live[("z", b)]
-            if VA and w in (BATCHES * TILES - 1, BATCHES * TILES - 3):
+            v = live[("v", w)]
+            ratio = live[("ratio", b)]
+            if engine is nc.scalar:
                 for n in range(HEADS):
-                    nc.scalar.activation(out=z[:, j, n * HEAD_DIM : (n + 1) * HEAD_DIM], in_=live[("v", w)][:, n * HEAD_DIM : (n + 1) * HEAD_DIM], func=ACT.Copy, scale=live[("ratio", b)][:, j, n : n + 1])
+                    features = slice(n * HEAD_DIM, (n + 1) * HEAD_DIM)
+                    nc.scalar.activation(
+                        out=z[:, j, features], in_=v[:, features], func=ACT.Copy, scale=ratio[:, j, n : n + 1]
+                    )
             else:
-              nc.vector.tensor_tensor(
-                out=z[:, j, :].rearrange("r (n d) -> r n d", n=HEADS),
-                in0=live[("v", w)][:].rearrange("r (n d) -> r n d", n=HEADS),
-                in1=live[("ratio", b)][:, j, :].unsqueeze(2).to_broadcast([P, HEADS, HEAD_DIM]),
-                op=ALU.mult,
-            )
-            if TAILS and b >= BATCHES - 1:
+                nc.vector.tensor_tensor(
+                    out=z[:, j, :].rearrange("r (n d) -> r n d", n=HEADS),
+                    in0=v[:].rearrange("r (n d) -> r n d", n=HEADS),
+                    in1=ratio[:, j, :].unsqueeze(2).to_broadcast([P, HEADS, HEAD_DIM]),
+                    op=ALU.mult,
+                )
+            if b >= BATCHES - 2:
                 nc.sync.dma_start(out=out[b].rearrange("(r j) f -> r j f", j=TILES)[:, j], in_=z[:, j, :])
             elif j == TILES - 1:
                 nc.sync.dma_start(
@@ -366,92 +309,83 @@ def tile_gatedlinearattention_pa_t_kernel(tc, hidden_states, Wq, Wk, Wv, out):
                 )
 
         transpose_x(0)
-        regroup(wk_raw, wk_grouped, 0, "vector")
-        regroup(wk_raw, wk_grouped, 1, "vector")
+        copy_x(0)
+        regroup(wk_raw, wk_grouped, 0, nc.vector)
+        regroup(wk_raw, wk_grouped, 1, nc.vector)
         quantise_x(0)
-        quantise_half(wk_grouped, wk_codes, wk_scales, 0)
-        regroup(wq_raw, wq_grouped, 0, "vector")
-        regroup(wq_raw, wq_grouped, 1, HQ)
-        quantise_half(wq_grouped, wq_codes, wq_scales, 0)
-        regroup(wk_raw, wk_grouped, 2, HB)
-        regroup(wk_raw, wk_grouped, 3, HB)
+        quantise_unit(wk_grouped, wk_codes, wk_scales, 0)
+        regroup(wq_raw, wq_grouped, 0, nc.vector)
+        regroup(wq_raw, wq_grouped, 1, nc.scalar)
+        quantise_unit(wq_grouped, wq_codes, wq_scales, 0)
+        regroup(wk_raw, wk_grouped, 2, nc.gpsimd)
+        regroup(wk_raw, wk_grouped, 3, nc.gpsimd)
 
-        for s in range(UNITS + VALUE_LAG):
-            if s < UNITS:
-                project(s)
-                if AORD == 0:
-                    relu_a(s)
-                    feature_c(s)
-                    exp_a(s)
-                elif AORD == 1:
-                    feature_c(s)
-                    relu_a(s)
-                elif AORD == 2:
-                    feature_c(s)
-                    relu_a(s)
-                    exp_a(s)
-                elif AORD == 3:
-                    if s:
-                        exp_a(s - 1)
-                    feature_c(s)
-                    relu_a(s)
-            elif AORD == 3 and s == UNITS:
-                exp_a(s - 1)
+        for s in range(UNITS):
+            project(s, "c", c_psum, wk_codes, wk_scales)
+            project(s, "a", a_psum, wq_codes, wq_scales)
+            decay_of_c(s)
+            below_a(s)
             if s == 0:
-                regroup(wq_raw, wq_grouped, 2, "vector")
-                regroup(wq_raw, wq_grouped, 3, "vector")
-                quantise_half(wk_grouped, wk_codes, wk_scales, 1)
-                quantise_half(wq_grouped, wq_codes, wq_scales, 1)
-            w = s - VALUE_LAG
-            if w >= 0:
-                project_v(w)
-                if not V_LAST:
-                    scale_v(w)
-            h = s - SUMS_LAG
-            if 0 <= h < UNITS:
-                if SUM_SPLIT:
-                    head_sums(*divmod(h, TILES))
-                elif h % 2 == 0:
-                    head_sums(h // 2, 0)
-                    head_sums(h // 2, 1)
-            if 1 <= s <= UNITS:
-                weigh(s - 1)
-            if AORD == 1 and s < UNITS:
-                exp_a(s)
-            if 1 <= s <= UNITS:
-                multiply(s - 1)
-            rb, rp = divmod(s - SUMS_LAG - RATIO_LAG - (TILES - 1 if SUM_SPLIT else 0), TILES)
-            divided = 0 <= rb < BATCHES and rp == 0
-            if divided and RECIP_LATE:
-                invert(rb)
-            if 0 <= s - CLAG < UNITS:
-                if QFIRST:
-                    make_q(s - CLAG)
-                    if divided:
-                        make_ratio(rb)
-                    make_k(s - CLAG)
-                else:
-                    make_k(s - CLAG)
-                    if divided:
-                        make_ratio(rb)
-                    make_q(s - CLAG)
-            elif divided:
-                make_ratio(rb)
-            if w >= 0 and V_LAST:
-                scale_v(w)
-            if 0 <= h < UNITS and h % TILES == (TILES - 1 if SUM_SPLIT else 0):
-                divide(h // TILES)
+                regroup(wq_raw, wq_grouped, 2, nc.vector)
+                regroup(wq_raw, wq_grouped, 3, nc.vector)
+                quantise_unit(wk_grouped, wk_codes, wk_scales, 1)
+                quantise_unit(wq_grouped, wq_codes, wq_scales, 1)
+            b, phase = divmod(s - SUMS_LAG, BATCH_UNITS)
+            if b >= 0 and phase == 0:
+                sum_heads(b)
+                reduce_sums(b)
+            if s >= WEIGH_LAG:
+                weigh(s - WEIGH_LAG)
+            decay_of_a(s)
+            b, phase = divmod(s - RATIO_LAG, BATCH_UNITS)
+            divided = b >= 0 and phase == 0
+            if divided:
+                invert(b)
+            if s >= VALUE_LAG:
+                project_v(s - VALUE_LAG)
+                scale_v(s - VALUE_LAG, nc.vector)
+            combine(s)
+            if s >= PRODUCT_LAG:
+                multiply(s - PRODUCT_LAG, nc.gpsimd)
+            if s == 0:
+                transpose_x(1)
+                copy_x(1)
+                quantise_x(1)
             if s == 3:
                 regroup_wv()
             if s == 4:
                 quantise(wv_grouped[:], wv_codes[:], wv_scales[:])
-            b, phase = divmod(s + XPREP, 2)
-            if s == 0:
-                for c in range(1, b):
-                    transpose_x(c)
-                    quantise_x(c)
-            if b < BATCHES:
+            x_batch, phase = divmod(s + X_LEAD, BATCH_UNITS)
+            if x_batch < BATCHES:
                 if phase == 0:
-                    transpose_x(b)
+                    transpose_x(x_batch)
+                    copy_x(x_batch)
                 else:
-                    quantise_x(b)
+                    quantise_x(x_batch)
+            if divided:
+                divide(b)
+
+        before_last, last = BATCHES - 2, BATCHES - 1
+        sum_heads(before_last)
+        reduce_sums(before_last)
+        weigh(UNITS - 2)
+        weigh(UNITS - 1)
+        multiply(UNITS - 1, nc.vector)
+        project_v(VALUES - 6)
+        project_v(VALUES - 5)
+        sum_heads(last)
+        invert(before_last)
+        scale_v(VALUES - 6, nc.vector)
+        divide(before_last)
+        scale_v(VALUES - 5, nc.scalar)
+        project_v(VALUES - 4)
+        project_v(VALUES - 3)
+        scale_v(VALUES - 4, nc.vector)
+        reduce_sums(last)
+        invert(last)
+        scale_v(VALUES - 3, nc.scalar)
+        divide(last)
+        project_v(VALUES - 2)
+        project_v(VALUES - 1)
+        scale_v(VALUES - 2, nc.vector)
+        scale_v(VALUES - 1, nc.vector)

@@ -27,6 +27,7 @@ VALUES = BATCHES * TILES
 
 PRODUCT_LAG = 1
 WEIGH_LAG = 2
+PRODUCT_SUMS_LAG = 3
 SUMS_LAG = 4
 RATIO_LAG = 5
 VALUE_LAG = 6
@@ -226,22 +227,23 @@ def tile_gatedlinearattention_pa_t_kernel(tc, hidden_states, Wq, Wk, Wv, out):
                 )
             live[("weighted", s)] = weighted
 
-        def sum_heads(b):
-            sums = sums_psum.tile([P, 2, TILES, P], F32)
-            for which, name in enumerate(("weighted", "product")):
-                for j in range(TILES):
-                    for slab in range(SLABS):
-                        h, i = divmod(slab, UNIT_SLABS)
-                        first = i * TOKENS + j * P
-                        nc.tensor.matmul(
-                            out=sums[:, which, j, :],
-                            lhsT=live[(name, b * BATCH_UNITS + h)][:, first : first + P],
-                            rhs=identity[:],
-                            is_transpose=True,
-                            start=(slab == 0),
-                            stop=(slab == SLABS - 1),
-                        )
-            live[("sums", b)] = sums
+        def sum_heads(b, name):
+            which = ("weighted", "product").index(name)
+            if name == "product":
+                sums = sums_psum.tile([P, 2, TILES, P], F32)
+                live[("sums", b)] = sums
+            for j in range(TILES):
+                for slab in range(SLABS):
+                    h, i = divmod(slab, UNIT_SLABS)
+                    first = i * TOKENS + j * P
+                    nc.tensor.matmul(
+                        out=live[("sums", b)][:, which, j, :],
+                        lhsT=live[(name, b * BATCH_UNITS + h)][:, first : first + P],
+                        rhs=identity[:],
+                        is_transpose=True,
+                        start=(slab == 0),
+                        stop=(slab == SLABS - 1),
+                    )
 
         def reduce_sums(b):
             totals = stage.tile([P, 2, TILES, HEADS], F32)
@@ -330,9 +332,12 @@ def tile_gatedlinearattention_pa_t_kernel(tc, hidden_states, Wq, Wk, Wv, out):
                 regroup(wq_raw, wq_grouped, 3, nc.vector)
                 quantise_unit(wk_grouped, wk_codes, wk_scales, 1)
                 quantise_unit(wq_grouped, wq_codes, wq_scales, 1)
+            b, phase = divmod(s - PRODUCT_SUMS_LAG, BATCH_UNITS)
+            if b >= 0 and phase == 0:
+                sum_heads(b, "product")
             b, phase = divmod(s - SUMS_LAG, BATCH_UNITS)
             if b >= 0 and phase == 0:
-                sum_heads(b)
+                sum_heads(b, "weighted")
                 reduce_sums(b)
             if s >= WEIGH_LAG:
                 weigh(s - WEIGH_LAG)
@@ -366,14 +371,15 @@ def tile_gatedlinearattention_pa_t_kernel(tc, hidden_states, Wq, Wk, Wv, out):
                 divide(b)
 
         before_last, last = BATCHES - 2, BATCHES - 1
-        sum_heads(before_last)
+        sum_heads(before_last, "weighted")
         reduce_sums(before_last)
         weigh(UNITS - 2)
         weigh(UNITS - 1)
         multiply(UNITS - 1, nc.vector)
         project_v(VALUES - 6)
         project_v(VALUES - 5)
-        sum_heads(last)
+        sum_heads(last, "product")
+        sum_heads(last, "weighted")
         invert(before_last)
         scale_v(VALUES - 6, nc.vector)
         divide(before_last)

@@ -25,12 +25,11 @@ UNITS = BATCHES * BATCH_UNITS
 UNIT_COLUMNS = UNIT_SLABS * TOKENS
 VALUES = BATCHES * TILES
 
-PRODUCT_LAG = 1
+PRODUCT_LAG = 2
 WEIGH_LAG = 2
-PRODUCT_SUMS_LAG = 3
 SUMS_LAG = 4
 RATIO_LAG = 5
-VALUE_LAG = 6
+VALUE_LAG = 7
 X_LEAD = 4
 
 FLOPS = 3 * 2 * BATCHES * TOKENS * HIDDEN * HIDDEN
@@ -41,10 +40,10 @@ def tile_gatedlinearattention_pa_t_kernel(tc, hidden_states, Wq, Wk, Wv, out):
     with ExitStack() as stack:
         keep = stack.enter_context(tc.tile_pool(name="keep", bufs=1))
         stage = stack.enter_context(tc.tile_pool(name="stage", bufs=3))
-        work = stack.enter_context(tc.tile_pool(name="work", bufs=4))
+        work = stack.enter_context(tc.tile_pool(name="work", bufs=5))
         c_psum = stack.enter_context(tc.psum_pool(name="c_psum", bufs=2))
-        a_psum = stack.enter_context(tc.psum_pool(name="a_psum", bufs=3))
-        aux_psum = stack.enter_context(tc.psum_pool(name="aux_psum", bufs=2))
+        a_psum = stack.enter_context(tc.psum_pool(name="a_psum", bufs=2))
+        aux_psum = stack.enter_context(tc.psum_pool(name="aux_psum", bufs=3))
         sums_psum = stack.enter_context(tc.psum_pool(name="sums_psum", bufs=1))
         stack.enter_context(tc.manual_schedule())
 
@@ -323,6 +322,12 @@ def tile_gatedlinearattention_pa_t_kernel(tc, hidden_states, Wq, Wk, Wv, out):
         regroup(wk_raw, wk_grouped, 3, nc.gpsimd)
 
         for s in range(UNITS):
+            if s >= PRODUCT_LAG:
+                multiply(s - PRODUCT_LAG, nc.gpsimd)
+            summed, phase = divmod(s - SUMS_LAG, BATCH_UNITS)
+            summing = summed >= 0 and phase == 0
+            if summing:
+                sum_heads(summed, "product")
             project(s, "c", c_psum, wk_codes, wk_scales)
             project(s, "a", a_psum, wq_codes, wq_scales)
             decay_of_c(s)
@@ -332,13 +337,9 @@ def tile_gatedlinearattention_pa_t_kernel(tc, hidden_states, Wq, Wk, Wv, out):
                 regroup(wq_raw, wq_grouped, 3, nc.vector)
                 quantise_unit(wk_grouped, wk_codes, wk_scales, 1)
                 quantise_unit(wq_grouped, wq_codes, wq_scales, 1)
-            b, phase = divmod(s - PRODUCT_SUMS_LAG, BATCH_UNITS)
-            if b >= 0 and phase == 0:
-                sum_heads(b, "product")
-            b, phase = divmod(s - SUMS_LAG, BATCH_UNITS)
-            if b >= 0 and phase == 0:
-                sum_heads(b, "weighted")
-                reduce_sums(b)
+            if summing:
+                sum_heads(summed, "weighted")
+                reduce_sums(summed)
             if s >= WEIGH_LAG:
                 weigh(s - WEIGH_LAG)
             decay_of_a(s)
@@ -350,8 +351,6 @@ def tile_gatedlinearattention_pa_t_kernel(tc, hidden_states, Wq, Wk, Wv, out):
                 project_v(s - VALUE_LAG)
                 scale_v(s - VALUE_LAG, nc.vector)
             combine(s)
-            if s >= PRODUCT_LAG:
-                multiply(s - PRODUCT_LAG, nc.gpsimd)
             if s == 0:
                 transpose_x(1)
                 copy_x(1)
@@ -371,27 +370,28 @@ def tile_gatedlinearattention_pa_t_kernel(tc, hidden_states, Wq, Wk, Wv, out):
                 divide(b)
 
         before_last, last = BATCHES - 2, BATCHES - 1
-        sum_heads(before_last, "weighted")
-        reduce_sums(before_last)
+        multiply(UNITS - 2, nc.gpsimd)
+        multiply(UNITS - 1, nc.vector)
         weigh(UNITS - 2)
         weigh(UNITS - 1)
-        multiply(UNITS - 1, nc.vector)
-        project_v(VALUES - 6)
-        project_v(VALUES - 5)
+        sum_heads(before_last, "product")
+        sum_heads(before_last, "weighted")
+        reduce_sums(before_last)
+        for w in range(VALUES - 7, VALUES - 4):
+            project_v(w)
+        scale_v(VALUES - 7, nc.vector)
         sum_heads(last, "product")
         sum_heads(last, "weighted")
         invert(before_last)
         scale_v(VALUES - 6, nc.vector)
-        divide(before_last)
         scale_v(VALUES - 5, nc.scalar)
-        project_v(VALUES - 4)
-        project_v(VALUES - 3)
-        scale_v(VALUES - 4, nc.vector)
+        divide(before_last)
+        for w in range(VALUES - 4, VALUES):
+            project_v(w)
         reduce_sums(last)
+        scale_v(VALUES - 4, nc.vector)
         invert(last)
         scale_v(VALUES - 3, nc.scalar)
         divide(last)
-        project_v(VALUES - 2)
-        project_v(VALUES - 1)
         scale_v(VALUES - 2, nc.vector)
         scale_v(VALUES - 1, nc.vector)

@@ -147,7 +147,7 @@ def tile_gatedlinearattention_pa_t_kernel(tc, hidden_states, Wq, Wk, Wv, out):
         def project(s, name, psum, codes, scales):
             b, h = divmod(s, BATCH_UNITS)
             tokens = slice(b * TOKENS, (b + 1) * TOKENS)
-            acc = psum.tile([P, UNIT_COLUMNS], F32, name="acc_" + name)
+            acc = psum.tile([P, UNIT_COLUMNS], F32, tag="acc_" + name)
             for i in range(UNIT_SLABS):
                 slab = h * UNIT_SLABS + i
                 columns = slice(slab * P, (slab + 1) * P)
@@ -226,49 +226,52 @@ def tile_gatedlinearattention_pa_t_kernel(tc, hidden_states, Wq, Wk, Wv, out):
                 )
             live[("weighted", s)] = weighted
 
-        def sum_heads(b, name):
-            which = ("weighted", "product").index(name)
+        def sum_heads(b, j, name, out):
+            for slab in range(SLABS):
+                h, i = divmod(slab, UNIT_SLABS)
+                first = i * TOKENS + j * P
+                nc.tensor.matmul(
+                    out=out,
+                    lhsT=live[(name, b * BATCH_UNITS + h)][:, first : first + P],
+                    rhs=identity[:],
+                    is_transpose=True,
+                    start=(slab == 0),
+                    stop=(slab == SLABS - 1),
+                )
+
+        def sum_batch(b, name):
             if name == "product":
                 sums = sums_psum.tile([P, 2, TILES, P], F32)
                 live[("sums", b)] = sums
+            which = ("weighted", "product").index(name)
             for j in range(TILES):
-                for slab in range(SLABS):
-                    h, i = divmod(slab, UNIT_SLABS)
-                    first = i * TOKENS + j * P
-                    nc.tensor.matmul(
-                        out=live[("sums", b)][:, which, j, :],
-                        lhsT=live[(name, b * BATCH_UNITS + h)][:, first : first + P],
-                        rhs=identity[:],
-                        is_transpose=True,
-                        start=(slab == 0),
-                        stop=(slab == SLABS - 1),
-                    )
+                sum_heads(b, j, name, live[("sums", b)][:, which, j, :])
 
-        def reduce_sums(b):
-            totals = stage.tile([P, 2, TILES, HEADS], F32)
+        def reduce_sums(key, tiles, sums):
+            totals = stage.tile([P, 2, tiles * HEADS], F32)
             nc.vector.tensor_reduce(
-                out=totals[:].rearrange("r w j n -> r (w j n)"),
-                in_=live[("sums", b)][:].rearrange("r w j (n e) -> r (w j n) e", n=HEADS),
+                out=totals[:].rearrange("r w h -> r (w h)"),
+                in_=sums.rearrange("r w j (n e) -> r (w j n) e", n=HEADS),
                 axis=mybir.AxisListType.X,
                 op=ALU.add,
             )
-            live[("totals", b)] = totals
+            live[("totals", key)] = totals
 
-        def invert(b):
-            inverse = stage.tile([P, TILES, HEADS], F32)
-            nc.vector.reciprocal(out=inverse[:], in_=live[("totals", b)][:, 0])
-            live[("inverse", b)] = inverse
+        def invert(key, tiles):
+            inverse = stage.tile([P, tiles * HEADS], F32)
+            nc.vector.reciprocal(out=inverse[:], in_=live[("totals", key)][:, 0])
+            live[("inverse", key)] = inverse
 
-        def divide(b):
-            ratio = stage.tile([P, TILES, HEADS], F32)
+        def divide(key, tiles):
+            ratio = stage.tile([P, tiles * HEADS], F32)
             nc.vector.tensor_tensor(
-                out=ratio[:], in0=live[("totals", b)][:, 1], in1=live[("inverse", b)][:], op=ALU.mult
+                out=ratio[:], in0=live[("totals", key)][:, 1], in1=live[("inverse", key)][:], op=ALU.mult
             )
-            live[("ratio", b)] = ratio
+            live[("ratio", key)] = ratio
 
-        def project_v(w):
+        def project_v(w, psum, tag):
             tokens = slice(w * P, (w + 1) * P)
-            v = aux_psum.tile([P, HIDDEN], F32, tag="aux")
+            v = psum.tile([P, HIDDEN], F32, tag=tag)
             nc.tensor.matmul_mx(
                 out=v[:],
                 lhsT=x_codes[:, tokens].bitcast(FP8X4),
@@ -280,28 +283,31 @@ def tile_gatedlinearattention_pa_t_kernel(tc, hidden_states, Wq, Wk, Wv, out):
             )
             live[("v", w)] = v
 
-        def scale_v(w, engine):
+        def scale_v(w, engine, key=None):
             b, j = divmod(w, TILES)
             if j == 0:
                 z = work.tile([P, TILES, HIDDEN], F32)
                 live[("z", b)] = z
             z = live[("z", b)]
             v = live[("v", w)]
-            ratio = live[("ratio", b)]
+            if key is None:
+                ratio = live[("ratio", b)][:, j * HEADS : (j + 1) * HEADS]
+            else:
+                ratio = live[("ratio", key)][:]
             if engine is nc.scalar:
                 for n in range(HEADS):
                     features = slice(n * HEAD_DIM, (n + 1) * HEAD_DIM)
                     nc.scalar.activation(
-                        out=z[:, j, features], in_=v[:, features], func=ACT.Copy, scale=ratio[:, j, n : n + 1]
+                        out=z[:, j, features], in_=v[:, features], func=ACT.Copy, scale=ratio[:, n : n + 1]
                     )
             else:
                 nc.vector.tensor_tensor(
                     out=z[:, j, :].rearrange("r (n d) -> r n d", n=HEADS),
                     in0=v[:].rearrange("r (n d) -> r n d", n=HEADS),
-                    in1=ratio[:, j, :].unsqueeze(2).to_broadcast([P, HEADS, HEAD_DIM]),
+                    in1=ratio.unsqueeze(2).to_broadcast([P, HEADS, HEAD_DIM]),
                     op=ALU.mult,
                 )
-            if b >= BATCHES - 2:
+            if b >= BATCHES - 4:
                 nc.sync.dma_start(out=out[b].rearrange("(r j) f -> r j f", j=TILES)[:, j], in_=z[:, j, :])
             elif j == TILES - 1:
                 nc.sync.dma_start(
@@ -327,7 +333,7 @@ def tile_gatedlinearattention_pa_t_kernel(tc, hidden_states, Wq, Wk, Wv, out):
             summed, phase = divmod(s - SUMS_LAG, BATCH_UNITS)
             summing = summed >= 0 and phase == 0
             if summing:
-                sum_heads(summed, "product")
+                sum_batch(summed, "product")
             project(s, "c", c_psum, wk_codes, wk_scales)
             project(s, "a", a_psum, wq_codes, wq_scales)
             decay_of_c(s)
@@ -338,17 +344,17 @@ def tile_gatedlinearattention_pa_t_kernel(tc, hidden_states, Wq, Wk, Wv, out):
                 quantise_unit(wk_grouped, wk_codes, wk_scales, 1)
                 quantise_unit(wq_grouped, wq_codes, wq_scales, 1)
             if summing:
-                sum_heads(summed, "weighted")
-                reduce_sums(summed)
+                sum_batch(summed, "weighted")
+                reduce_sums(summed, TILES, live[("sums", summed)][:])
             if s >= WEIGH_LAG:
                 weigh(s - WEIGH_LAG)
             decay_of_a(s)
             b, phase = divmod(s - RATIO_LAG, BATCH_UNITS)
             divided = b >= 0 and phase == 0
             if divided:
-                invert(b)
+                invert(b, TILES)
             if s >= VALUE_LAG:
-                project_v(s - VALUE_LAG)
+                project_v(s - VALUE_LAG, aux_psum, "aux")
                 scale_v(s - VALUE_LAG, nc.vector)
             combine(s)
             if s == 0:
@@ -367,31 +373,41 @@ def tile_gatedlinearattention_pa_t_kernel(tc, hidden_states, Wq, Wk, Wv, out):
                 else:
                     quantise_x(x_batch)
             if divided:
-                divide(b)
+                divide(b, TILES)
 
         before_last, last = BATCHES - 2, BATCHES - 1
+        project_v(VALUES - 7, aux_psum, "aux")
+        project_v(VALUES - 6, aux_psum, "aux")
         multiply(UNITS - 2, nc.gpsimd)
         multiply(UNITS - 1, nc.vector)
         weigh(UNITS - 2)
         weigh(UNITS - 1)
-        sum_heads(before_last, "product")
-        sum_heads(before_last, "weighted")
-        reduce_sums(before_last)
-        for w in range(VALUES - 7, VALUES - 4):
-            project_v(w)
+        sum_batch(before_last, "product")
+        sum_batch(before_last, "weighted")
+        reduce_sums(before_last, TILES, live[("sums", before_last)][:])
+        project_v(VALUES - 5, aux_psum, "aux")
+        project_v(VALUES - 4, a_psum, "acc_a")
+        project_v(VALUES - 3, a_psum, "acc_a")
+        tile_sums = []
+        for j in range(TILES):
+            tile_sum = c_psum.tile([P, 2, 1, P], F32, tag="acc_c")
+            sum_heads(last, j, "product", tile_sum[:, 1, 0, :])
+            sum_heads(last, j, "weighted", tile_sum[:, 0, 0, :])
+            tile_sums.append(tile_sum)
         scale_v(VALUES - 7, nc.vector)
-        sum_heads(last, "product")
-        sum_heads(last, "weighted")
-        invert(before_last)
-        scale_v(VALUES - 6, nc.vector)
+        scale_v(VALUES - 6, nc.scalar)
         scale_v(VALUES - 5, nc.scalar)
-        divide(before_last)
-        for w in range(VALUES - 4, VALUES):
-            project_v(w)
-        reduce_sums(last)
+        project_v(VALUES - 2, aux_psum, "aux")
+        project_v(VALUES - 1, aux_psum, "aux")
+        invert(before_last, TILES)
+        reduce_sums("first", 1, tile_sums[0][:])
+        divide(before_last, TILES)
+        invert("first", 1)
+        reduce_sums("second", 1, tile_sums[1][:])
         scale_v(VALUES - 4, nc.vector)
-        invert(last)
+        divide("first", 1)
+        invert("second", 1)
         scale_v(VALUES - 3, nc.scalar)
-        divide(last)
-        scale_v(VALUES - 2, nc.vector)
-        scale_v(VALUES - 1, nc.vector)
+        divide("second", 1)
+        scale_v(VALUES - 2, nc.vector, "first")
+        scale_v(VALUES - 1, nc.vector, "second")

from contextlib import ExitStack

import concourse.mybir as mybir
from concourse.masks import make_identity

F32 = mybir.dt.float32
BF16 = mybir.dt.bfloat16
U32 = mybir.dt.uint32
U8 = mybir.dt.uint8
FP8X4 = mybir.dt.float8_e4m3fn_x4
ALU = mybir.AluOpType
ACT = mybir.ActivationFunctionType

P = 128
PACK = 4
BATCHES, TOKENS, HIDDEN, HEADS = 16, 256, 512, 8
HEAD_DIM = HIDDEN // HEADS
NORM_EPS = 1e-6

TILES = TOKENS // P
SLABS = HIDDEN // P
UNIT_SLABS = 2
BATCH_UNITS = SLABS // UNIT_SLABS
UNITS = BATCHES * BATCH_UNITS
UNIT_COLUMNS = UNIT_SLABS * TOKENS
VALUES = BATCHES * TILES

PRODUCT_LAG = 2
WEIGH_LAG = 2
SUMS_LAG = 4
RATIO_LAG = 5
VALUE_LAG = 7
X_LEAD = 4

FLOPS = 3 * 2 * BATCHES * TOKENS * HIDDEN * HIDDEN


def tile_gatedlinearattention_pa_t_kernel(tc, hidden_states, Wq, Wk, Wv, out):
    nc = tc.nc
    with ExitStack() as stack:
        keep = stack.enter_context(tc.tile_pool(name="keep", bufs=1))
        stage = stack.enter_context(tc.tile_pool(name="stage", bufs=3))
        work = stack.enter_context(tc.tile_pool(name="work", bufs=5))
        c_psum = stack.enter_context(tc.psum_pool(name="c_psum", bufs=2))
        a_psum = stack.enter_context(tc.psum_pool(name="a_psum", bufs=2))
        aux_psum = stack.enter_context(tc.psum_pool(name="aux_psum", bufs=3))
        sums_psum = stack.enter_context(tc.psum_pool(name="sums_psum", bufs=1))
        stack.enter_context(tc.manual_schedule())

        x_raw = keep.tile([P, BATCHES, TILES * HIDDEN], BF16)

        def load_x(first, count):
            nc.sync.dma_start(
                out=x_raw[:, first : first + count, :],
                in_=hidden_states[first : first + count].rearrange("b (r j) k -> r b (j k)", j=TILES),
            )

        def load_weight(w, raw):
            nc.sync.dma_start(out=raw[:], in_=w.rearrange("(p t) n -> p (t n)", t=PACK))

        wq_raw = keep.tile([P, PACK * HIDDEN], BF16)
        wk_raw = keep.tile([P, PACK * HIDDEN], BF16)
        wv_raw = keep.tile([P, PACK * HIDDEN], BF16)
        load_x(0, 1)
        load_weight(Wk, wk_raw)
        load_weight(Wq, wq_raw)
        load_x(1, 1)
        load_x(2, 2)
        load_weight(Wv, wv_raw)
        for b in range(4, BATCHES, 4):
            load_x(b, 4)

        identity = keep.tile([P, P], F32)
        make_identity(nc, identity[:])
        table_warmer = keep.tile([P, 1], F32)
        nc.vector.memset(table_warmer[:], 0.0)
        nc.scalar.activation(out=table_warmer[:], in_=table_warmer[:], func=ACT.Exp)

        wq_grouped = keep.tile([P, HIDDEN * PACK], BF16, align_bytes=64)
        wk_grouped = keep.tile([P, HIDDEN * PACK], BF16, align_bytes=64)
        wv_grouped = keep.tile([P, HIDDEN * PACK], BF16, align_bytes=64)
        wq_codes = keep.tile([P, HIDDEN], U32, align_bytes=64)
        wk_codes = keep.tile([P, HIDDEN], U32, align_bytes=64)
        wv_codes = keep.tile([P, HIDDEN], U32, align_bytes=64)
        wq_scales = keep.tile([P, HIDDEN], U8, align_bytes=64)
        wk_scales = keep.tile([P, HIDDEN], U8, align_bytes=64)
        wv_scales = keep.tile([P, HIDDEN], U8, align_bytes=64)
        x_codes = keep.tile([P, BATCHES * TOKENS], U32, align_bytes=64)
        x_scales = keep.tile([P, BATCHES * TOKENS], U8, align_bytes=64)

        def quantise(grouped, codes, scales):
            nc.vector.quantize_mx(out=codes.bitcast(FP8X4), scales=scales, in_=grouped)

        def regroup(raw, grouped, i, engine):
            elements = slice(i * P * PACK, (i + 1) * P * PACK)
            words = grouped[:, elements].rearrange("p (n e t) -> p n e t", n=HEADS, t=PACK)
            columns = raw[:].rearrange("p (t n i e) -> p i n e t", t=PACK, n=HEADS, i=SLABS)[:, i]
            if engine is nc.scalar:
                nc.scalar.copy(out=words, in_=columns)
            elif engine is nc.gpsimd:
                nc.gpsimd.tensor_scalar(
                    out=words, in0=columns, scalar1=1.0, scalar2=0.0, op0=ALU.mult, op1=ALU.add
                )
            else:
                nc.vector.tensor_copy(out=words, in_=columns)

        def quantise_unit(grouped, codes, scales, h):
            columns = slice(h * UNIT_SLABS * P, (h + 1) * UNIT_SLABS * P)
            elements = slice(h * UNIT_SLABS * P * PACK, (h + 1) * UNIT_SLABS * P * PACK)
            quantise(grouped[:, elements], codes[:, columns], scales[:, columns])

        def regroup_wv():
            nc.vector.tensor_copy(
                out=wv_grouped[:].rearrange("p (c i t) -> p c t i", i=4, t=PACK),
                in_=wv_raw[:].rearrange("p (t c i) -> p c t i", t=PACK, i=4),
            )

        live = {}

        def transpose_x(b):
            words = x_raw[:, b, :].bitcast(F32)
            token_words = HIDDEN // 2
            xt = aux_psum.tile([P, 2, TOKENS], F32, tag="aux")
            for j in range(TILES):
                for u in range(2):
                    nc.tensor.transpose(
                        xt[:, u, j * P : (j + 1) * P],
                        words[:, j * token_words + u : (j + 1) * token_words : 2],
                        identity[:],
                    )
            live[("xt", b)] = xt

        def copy_x(b):
            x_grouped = stage.tile([P, TOKENS * PACK], BF16, align_bytes=64)
            side_by_side = x_grouped[:].bitcast(F32).rearrange("p (c u) -> p c u", u=2)
            words = live[("xt", b)][:].rearrange("p u c -> p c u")
            if b % 2 == 0:
                nc.scalar.copy(out=side_by_side, in_=words)
            else:
                nc.vector.tensor_copy(out=side_by_side, in_=words)
            live[("x_grouped", b)] = x_grouped

        def quantise_x(b):
            tokens = slice(b * TOKENS, (b + 1) * TOKENS)
            quantise(live[("x_grouped", b)][:], x_codes[:, tokens], x_scales[:, tokens])

        def project(s, name, psum, codes, scales):
            b, h = divmod(s, BATCH_UNITS)
            tokens = slice(b * TOKENS, (b + 1) * TOKENS)
            acc = psum.tile([P, UNIT_COLUMNS], F32, tag="acc_" + name)
            for i in range(UNIT_SLABS):
                slab = h * UNIT_SLABS + i
                columns = slice(slab * P, (slab + 1) * P)
                nc.tensor.matmul_mx(
                    out=acc[:, i * TOKENS : (i + 1) * TOKENS],
                    lhsT=codes[:, columns].bitcast(FP8X4),
                    lhsT_scale=scales[:, columns],
                    rhs=x_codes[:, tokens].bitcast(FP8X4),
                    rhs_scale=x_scales[:, tokens],
                    start=True,
                    stop=True,
                )
            live[(name, s)] = acc

        def decay_of_c(s):
            exp_c = work.tile([P, UNIT_COLUMNS], F32)
            nc.scalar.activation(out=exp_c[:], in_=live[("c", s)][:], func=ACT.Exp)
            decay_c = work.tile([P, UNIT_COLUMNS], F32)
            nc.gpsimd.tensor_scalar(
                out=decay_c[:], in0=exp_c[:], scalar1=1.0, scalar2=0.0, op0=ALU.min, op1=ALU.max
            )
            live[("decay_c", s)] = decay_c

        def below_a(s):
            below = work.tile([P, UNIT_COLUMNS], F32)
            nc.scalar.activation(out=below[:], in_=live[("a", s)][:], func=ACT.Relu, scale=-1.0)
            live[("below", s)] = below

        def decay_of_a(s):
            decay_a = work.tile([P, UNIT_COLUMNS], F32)
            nc.scalar.activation(out=decay_a[:], in_=live[("below", s)][:], func=ACT.Exp, scale=-1.0)
            live[("decay_a", s)] = decay_a

        def combine(s):
            k = work.tile([P, UNIT_COLUMNS], F32)
            k_sum = work.tile([P, UNIT_SLABS], F32)
            for i in range(UNIT_SLABS):
                columns = slice(i * TOKENS, (i + 1) * TOKENS)
                nc.vector.scalar_tensor_tensor(
                    out=k[:, columns],
                    in0=live[("c", s)][:, columns],
                    scalar=0.0,
                    in1=live[("decay_c", s)][:, columns],
                    op0=ALU.max,
                    op1=ALU.add,
                    accum_out=k_sum[:, i : i + 1],
                )
            q = work.tile([P, UNIT_COLUMNS], F32)
            nc.vector.scalar_tensor_tensor(
                out=q[:],
                in0=live[("a", s)][:],
                scalar=0.0,
                in1=live[("decay_a", s)][:],
                op0=ALU.max,
                op1=ALU.add,
            )
            live[("k", s)] = k
            live[("k_sum", s)] = k_sum
            live[("q", s)] = q

        def multiply(s, engine):
            product = work.tile([P, UNIT_COLUMNS], F32)
            engine.tensor_tensor(out=product[:], in0=live[("q", s)][:], in1=live[("k", s)][:], op=ALU.mult)
            live[("product", s)] = product

        def weigh(s):
            weighted = work.tile([P, UNIT_COLUMNS], F32)
            for i in range(UNIT_SLABS):
                columns = slice(i * TOKENS, (i + 1) * TOKENS)
                nc.scalar.activation(
                    out=weighted[:, columns],
                    in_=live[("q", s)][:, columns],
                    func=ACT.Copy,
                    scale=live[("k_sum", s)][:, i : i + 1],
                    bias=NORM_EPS / HEAD_DIM,
                )
            live[("weighted", s)] = weighted

        def sum_heads(b, j, name, out):
            for slab in range(SLABS):
                h, i = divmod(slab, UNIT_SLABS)
                first = i * TOKENS + j * P
                nc.tensor.matmul(
                    out=out,
                    lhsT=live[(name, b * BATCH_UNITS + h)][:, first : first + P],
                    rhs=identity[:],
                    is_transpose=True,
                    start=(slab == 0),
                    stop=(slab == SLABS - 1),
                )

        def sum_batch(b, name):
            if name == "product":
                sums = sums_psum.tile([P, 2, TILES, P], F32)
                live[("sums", b)] = sums
            which = ("weighted", "product").index(name)
            for j in range(TILES):
                sum_heads(b, j, name, live[("sums", b)][:, which, j, :])

        def reduce_sums(key, tiles, sums):
            totals = stage.tile([P, 2, tiles * HEADS], F32)
            nc.vector.tensor_reduce(
                out=totals[:].rearrange("r w h -> r (w h)"),
                in_=sums.rearrange("r w j (n e) -> r (w j n) e", n=HEADS),
                axis=mybir.AxisListType.X,
                op=ALU.add,
            )
            live[("totals", key)] = totals

        def invert(key, tiles):
            inverse = stage.tile([P, tiles * HEADS], F32)
            nc.vector.reciprocal(out=inverse[:], in_=live[("totals", key)][:, 0])
            live[("inverse", key)] = inverse

        def divide(key, tiles):
            ratio = stage.tile([P, tiles * HEADS], F32)
            nc.vector.tensor_tensor(
                out=ratio[:], in0=live[("totals", key)][:, 1], in1=live[("inverse", key)][:], op=ALU.mult
            )
            live[("ratio", key)] = ratio

        def project_v(w, psum, tag):
            tokens = slice(w * P, (w + 1) * P)
            v = psum.tile([P, HIDDEN], F32, tag=tag)
            nc.tensor.matmul_mx(
                out=v[:],
                lhsT=x_codes[:, tokens].bitcast(FP8X4),
                lhsT_scale=x_scales[:, tokens],
                rhs=wv_codes[:].bitcast(FP8X4),
                rhs_scale=wv_scales[:],
                start=True,
                stop=True,
            )
            live[("v", w)] = v

        def scale_v(w, engine, key=None):
            b, j = divmod(w, TILES)
            if j == 0:
                z = work.tile([P, TILES, HIDDEN], F32)
                live[("z", b)] = z
            z = live[("z", b)]
            v = live[("v", w)]
            if key is None:
                ratio = live[("ratio", b)][:, j * HEADS : (j + 1) * HEADS]
            else:
                ratio = live[("ratio", key)][:]
            if engine is nc.scalar:
                for n in range(HEADS):
                    features = slice(n * HEAD_DIM, (n + 1) * HEAD_DIM)
                    nc.scalar.activation(
                        out=z[:, j, features], in_=v[:, features], func=ACT.Copy, scale=ratio[:, n : n + 1]
                    )
            else:
                nc.vector.tensor_tensor(
                    out=z[:, j, :].rearrange("r (n d) -> r n d", n=HEADS),
                    in0=v[:].rearrange("r (n d) -> r n d", n=HEADS),
                    in1=ratio.unsqueeze(2).to_broadcast([P, HEADS, HEAD_DIM]),
                    op=ALU.mult,
                )
            if b >= BATCHES - 4:
                nc.sync.dma_start(out=out[b].rearrange("(r j) f -> r j f", j=TILES)[:, j], in_=z[:, j, :])
            elif j == TILES - 1:
                nc.sync.dma_start(
                    out=out[b].rearrange("(r j) f -> r (j f)", j=TILES),
                    in_=z[:].rearrange("r j f -> r (j f)"),
                )

        transpose_x(0)
        copy_x(0)
        regroup(wk_raw, wk_grouped, 0, nc.vector)
        regroup(wk_raw, wk_grouped, 1, nc.vector)
        quantise_x(0)
        quantise_unit(wk_grouped, wk_codes, wk_scales, 0)
        regroup(wq_raw, wq_grouped, 0, nc.vector)
        regroup(wq_raw, wq_grouped, 1, nc.scalar)
        quantise_unit(wq_grouped, wq_codes, wq_scales, 0)
        regroup(wk_raw, wk_grouped, 2, nc.gpsimd)
        regroup(wk_raw, wk_grouped, 3, nc.gpsimd)

        for s in range(UNITS):
            if s >= PRODUCT_LAG:
                multiply(s - PRODUCT_LAG, nc.gpsimd)
            summed, phase = divmod(s - SUMS_LAG, BATCH_UNITS)
            summing = summed >= 0 and phase == 0
            if summing:
                sum_batch(summed, "product")
            project(s, "c", c_psum, wk_codes, wk_scales)
            project(s, "a", a_psum, wq_codes, wq_scales)
            decay_of_c(s)
            below_a(s)
            if s == 0:
                regroup(wq_raw, wq_grouped, 2, nc.vector)
                regroup(wq_raw, wq_grouped, 3, nc.vector)
                quantise_unit(wk_grouped, wk_codes, wk_scales, 1)
                quantise_unit(wq_grouped, wq_codes, wq_scales, 1)
            if summing:
                sum_batch(summed, "weighted")
                reduce_sums(summed, TILES, live[("sums", summed)][:])
            if s >= WEIGH_LAG:
                weigh(s - WEIGH_LAG)
            decay_of_a(s)
            b, phase = divmod(s - RATIO_LAG, BATCH_UNITS)
            divided = b >= 0 and phase == 0
            if divided:
                invert(b, TILES)
            if s >= VALUE_LAG:
                project_v(s - VALUE_LAG, aux_psum, "aux")
                scale_v(s - VALUE_LAG, nc.vector)
            combine(s)
            if s == 0:
                transpose_x(1)
                copy_x(1)
                quantise_x(1)
            if s == 3:
                regroup_wv()
            if s == 4:
                quantise(wv_grouped[:], wv_codes[:], wv_scales[:])
            x_batch, phase = divmod(s + X_LEAD, BATCH_UNITS)
            if x_batch < BATCHES:
                if phase == 0:
                    transpose_x(x_batch)
                    copy_x(x_batch)
                else:
                    quantise_x(x_batch)
            if divided:
                divide(b, TILES)

        before_last, last = BATCHES - 2, BATCHES - 1
        project_v(VALUES - 7, aux_psum, "aux")
        project_v(VALUES - 6, aux_psum, "aux")
        multiply(UNITS - 2, nc.gpsimd)
        multiply(UNITS - 1, nc.vector)
        weigh(UNITS - 2)
        weigh(UNITS - 1)
        sum_batch(before_last, "product")
        sum_batch(before_last, "weighted")
        reduce_sums(before_last, TILES, live[("sums", before_last)][:])
        project_v(VALUES - 5, aux_psum, "aux")
        project_v(VALUES - 4, a_psum, "acc_a")
        project_v(VALUES - 3, a_psum, "acc_a")
        tile_sums = []
        for j in range(TILES):
            tile_sum = c_psum.tile([P, 2, 1, P], F32, tag="acc_c")
            sum_heads(last, j, "product", tile_sum[:, 1, 0, :])
            sum_heads(last, j, "weighted", tile_sum[:, 0, 0, :])
            tile_sums.append(tile_sum)
        scale_v(VALUES - 7, nc.vector)
        scale_v(VALUES - 6, nc.scalar)
        scale_v(VALUES - 5, nc.scalar)
        project_v(VALUES - 2, aux_psum, "aux")
        project_v(VALUES - 1, aux_psum, "aux")
        invert(before_last, TILES)
        reduce_sums("first", 1, tile_sums[0][:])
        divide(before_last, TILES)
        invert("first", 1)
        reduce_sums("second", 1, tile_sums[1][:])
        scale_v(VALUES - 4, nc.vector)
        divide("first", 1)
        invert("second", 1)
        scale_v(VALUES - 3, nc.scalar)
        divide("second", 1)
        scale_v(VALUES - 2, nc.vector, "first")
        scale_v(VALUES - 1, nc.vector, "second")
